import numpy as np
import ml_dtypes


def mxq(x, axis, fmt="e4m3"):
    dtype, down = {"e4m3": (ml_dtypes.float8_e4m3fn, 7), "e5m2": (ml_dtypes.float8_e5m2, 14)}[fmt]
    v = np.moveaxis(np.asarray(x, np.float32).astype(ml_dtypes.bfloat16).astype(np.float64), axis, -1)
    blocks = v.reshape(v.shape[:-1] + (-1, 32))
    amax = np.abs(blocks).max(-1, keepdims=True)
    byte = np.maximum(np.where(amax > 0, np.frexp(amax)[1] - 1 + 127, 0) - down, 1)
    scale = np.exp2(byte - 127.0)
    codes = (blocks / scale).astype(np.float32).astype(dtype).astype(np.float64)
    return np.moveaxis((codes * scale).reshape(v.shape), -1, axis)


WIDE = False


def mx_kscale(k):
    if not WIDE:
        return np.ones(k)
    levels = np.array([10, -10, 5, -5, 0])
    a = np.random.permutation(np.resize(levels, k // 512 * 4)).reshape(k // 512, 4)
    idx = np.arange(k)
    return np.exp2(a[idx // 512, idx % 128 // 32])


BF16 = ml_dtypes.bfloat16


def bf(x):
    return np.asarray(x, np.float32).astype(BF16)


def f64(x):
    return np.asarray(x).astype(np.float64)


E2M1 = np.array([0.0, 0.5, 1.0, 1.5, 2.0, 3.0, 4.0, 6.0, -0.0, -0.5, -1.0, -1.5, -2.0, -3.0, -4.0, -6.0])


def pack_weight(w, fmt):
    k, n = w.shape
    w = f64(bf(w)).reshape(k // 32, 32, n)
    amax = np.abs(w).max(1)
    if fmt == "e4m3":
        byte = np.frexp(amax)[1] - 1 + 127 - 7
    else:
        mant, ex = np.frexp(amax / 6.0)
        byte = np.where(mant > 0.5, ex, ex - 1) + 127
    byte = np.clip(np.where(amax > 0, byte, 1), 1, 254)
    scaled = (w * np.exp2(127.0 - byte)[:, None, :]).reshape(k, n).astype(np.float32)
    by_word = np.ascontiguousarray(scaled.reshape(k // 512, 128, 4, n).transpose(0, 1, 3, 2))
    if fmt == "e4m3":
        words = by_word.astype(ml_dtypes.float8_e4m3fn).view(np.uint8)
    else:
        c = by_word.astype(ml_dtypes.float4_e2m1fn).view(np.uint8) & 0xF
        words = c[..., 0::2] | (c[..., 1::2] << 4)
    return np.ascontiguousarray(words), np.ascontiguousarray(byte.astype(np.uint8).reshape(k // 512, 16, n))


def unpack_weight(words, scales, fmt):
    g, p, n, _ = words.shape
    if fmt == "e4m3":
        vals = np.ascontiguousarray(words).view(ml_dtypes.float8_e4m3fn).astype(np.float64)
    else:
        nib = np.empty((g, p, n, 4), np.uint8)
        nib[..., 0::2] = words & 0xF
        nib[..., 1::2] = words >> 4
        vals = E2M1[nib]
    vals = vals * np.repeat(np.exp2(scales.astype(np.float64) - 127.0), 8, axis=1)[..., None]
    return vals.transpose(0, 1, 3, 2).reshape(g * 512, n)


NTR, NTE, D, C = 8192, 512, 512, 128
GAMMA = 10.0


def setup_inputs():
    s = mx_kscale(D)
    sM_words, sM_scales = pack_weight((np.random.standard_normal((NTR, D)) * s).T, "e4m3")
    x_test = bf(np.random.standard_normal((NTE, D)) / s)
    s_norm2 = bf(np.random.standard_normal(NTR) * np.sqrt(D))
    c_norm2 = bf(np.random.standard_normal(NTE) * np.sqrt(D))
    y_train_words, y_train_scales = pack_weight(np.random.standard_normal((NTR, C)) * 0.125 * np.sqrt(NTR), "e4m3")
    return {"sM_words": sM_words,
            "sM_scales": sM_scales,
            "x_test": x_test,
            "s_norm2": s_norm2,
            "c_norm2": c_norm2,
            "y_train_words": y_train_words,
            "y_train_scales": y_train_scales}


def reference(sM_words, sM_scales, x_test, s_norm2, c_norm2, y_train_words, y_train_scales):
    cross = unpack_weight(sM_words, sM_scales, "e4m3").T @ mxq(f64(x_test).T, 0, "e4m3")
    d2 = (-2.0) * cross + f64(s_norm2)[:, None] + f64(c_norm2)[None, :]
    dist = np.sqrt(np.clip(d2, 0.0, None))
    K = np.exp(dist * (-1.0 / GAMMA))
    Kt = K.T
    normalized = Kt / Kt.sum(axis=1, keepdims=True)
    return mxq(normalized, 1, "e4m3") @ unpack_weight(y_train_words, y_train_scales, "e4m3")

@@ -1,0 +1,264 @@
+from contextlib import ExitStack
+
+import concourse.mybir as mybir
+from concourse.masks import make_identity
+
+F32 = mybir.dt.float32
+BF16 = mybir.dt.bfloat16
+I32 = mybir.dt.int32
+U32 = mybir.dt.uint32
+U8 = mybir.dt.uint8
+FP8X4 = mybir.dt.float8_e4m3fn_x4
+ALU = mybir.AluOpType
+ACT = mybir.ActivationFunctionType
+
+P = 128
+PACK = 4
+K_PASS = P * PACK
+NTR, NTE, D, C = 8192, 512, 512, 128
+GAMMA = 10.0
+J_TILES = NTE // P
+GROUPS = NTR // K_PASS
+QUAD = 4
+CLAMP_COLS = 1024
+EXP_COLS = 2048
+WORD_LOAD_COLS = 1024
+SQRT_FLOOR = 2.0 ** -100
+
+FLOPS = 2 * NTR * NTE * D + 2 * NTE * NTR * C
+
+
+def tile_rbfnet_pb_t_kernel(
+    tc, sM_words, sM_scales, x_test, s_norm2, c_norm2, y_train_words, y_train_scales, out
+):
+    nc = tc.nc
+    with ExitStack() as ctx:
+        keep = ctx.enter_context(tc.tile_pool(name="keep", bufs=1))
+        work = ctx.enter_context(tc.tile_pool(name="work", bufs=2))
+        psum_cross = ctx.enter_context(tc.psum_pool(name="psum_cross", bufs=3))
+        psum_flip = ctx.enter_context(tc.psum_pool(name="psum_flip", bufs=3))
+        psum_one = ctx.enter_context(tc.psum_pool(name="psum_one", bufs=1))
+        ctx.enter_context(tc.manual_schedule())
+
+        x_sb = keep.tile([P, J_TILES, D], BF16)
+        x_grouped = keep.tile([P, NTE * PACK], BF16, align_bytes=64)
+        x_codes = keep.tile([P, NTE], U32, align_bytes=64)
+        x_planes = keep.tile([P, NTE], U8, align_bytes=64)
+        sm_codes = keep.tile([P, NTR], U32, align_bytes=64)
+        sm_planes = keep.tile([P, NTR], U8, align_bytes=64)
+        y_codes = keep.tile([P, GROUPS, C], U32, align_bytes=64)
+        y_planes = keep.tile([P, GROUPS, C], U8, align_bytes=64)
+        vec_rows = keep.tile([P, K_PASS], BF16)
+        s_cols = keep.tile([P, GROUPS, PACK], BF16)
+        c_cols = keep.tile([P, J_TILES], F32)
+        s_all = keep.tile([P, GROUPS, PACK, P], BF16)
+        ident_f32 = keep.tile([P, P], F32)
+        ident_bf16 = keep.tile([P, P], BF16)
+        warm = keep.tile([P, 2], F32)
+        k_sums = keep.tile([P, J_TILES, NTR // EXP_COLS], F32)
+        k_tiles = [keep.tile([P, NTR], F32, name="k_tile%d" % jt) for jt in range(J_TILES)]
+        out_acc = psum_one.tile([P, J_TILES, C], F32)
+
+        nc.vector.memset(sm_planes[:].bitcast(I32), 0)
+        nc.vector.memset(vec_rows[:], 0.0)
+        nc.vector.memset(warm[:], 1.0)
+        nc.vector.memset(y_planes[:].rearrange("p g c -> p (g c)").bitcast(I32), 0)
+        make_identity(nc, ident_f32[:])
+        make_identity(nc, ident_bf16[:])
+        nc.scalar.activation(out=warm[:, 1:2], in_=warm[:, 0:1], func=ACT.Sqrt)
+
+        nc.sync.dma_start(out=x_sb[:], in_=x_test.rearrange("(a p) k -> p a k", p=P))
+        nc.sync.dma_start(out=vec_rows[0:GROUPS, :], in_=s_norm2.rearrange("(g n) -> g n", g=GROUPS))
+        nc.sync.dma_start(
+            out=vec_rows[GROUPS : GROUPS + J_TILES, 0:P],
+            in_=c_norm2.rearrange("(a n) -> a n", a=J_TILES),
+        )
+        sm_scale_rows = sM_scales.rearrange("o q n -> (o q) n")
+        for half in range(2):
+            cols = slice(half * (NTR // 2), (half + 1) * (NTR // 2))
+            for b in range(2):
+                for r in range(4):
+                    nc.sync.dma_start(
+                        out=sm_planes[32 * b + r : P : 64, cols].bitcast(I32),
+                        in_=sm_scale_rows[4 * b + r : 16 : 8, cols].bitcast(I32),
+                    )
+        sm_word_bytes = sM_words.rearrange("o p n t -> (o p) (n t)")
+        for first in range(0, NTR, WORD_LOAD_COLS):
+            nc.sync.dma_start(
+                out=sm_codes[:, first : first + WORD_LOAD_COLS].bitcast(I32),
+                in_=sm_word_bytes[:, PACK * first : PACK * (first + WORD_LOAD_COLS)].bitcast(I32),
+            )
+        for quadrant in range(4):
+            nc.sync.dma_start(
+                out=y_planes[32 * quadrant : 32 * quadrant + 4, :, :].bitcast(I32),
+                in_=y_train_scales[:, 4 * quadrant : 4 * quadrant + 4, :]
+                .rearrange("g r n -> r g n")
+                .bitcast(I32),
+            )
+        nc.sync.dma_start(
+            out=y_codes[:].bitcast(I32),
+            in_=y_train_words.rearrange("g p n t -> p g (n t)").bitcast(I32),
+        )
+
+        x_grouped_words = x_grouped[:].bitcast(F32).rearrange("p (a j u) -> p a j u", a=J_TILES, u=2)
+        for pair in range(J_TILES // 2):
+            x_flip = psum_flip.tile([P, 2, 2, P], F32, tag="flip")
+            for a in range(2):
+                for u in range(2):
+                    nc.tensor.transpose(
+                        x_flip[:, a, u, :],
+                        x_sb[:, 2 * pair + a, :].bitcast(F32)[:, u : D // 2 : 2],
+                        ident_f32[:],
+                    )
+            nc.vector.tensor_copy(
+                out=x_grouped_words[:, 2 * pair : 2 * pair + 2, :, :],
+                in_=x_flip[:].rearrange("p a u j -> p a j u"),
+            )
+
+        vec_flip = psum_one.tile([P, PACK + 1, P], BF16, tag="small")
+        for t in range(PACK):
+            nc.tensor.transpose(vec_flip[:, t, :], vec_rows[:, t:K_PASS:PACK], ident_bf16[:])
+        nc.tensor.transpose(vec_flip[:, PACK, :], vec_rows[:, 0:P], ident_bf16[:])
+        nc.vector.tensor_copy(
+            out=s_cols[:], in_=vec_flip[:, 0:PACK, 0:GROUPS].rearrange("p t g -> p g t")
+        )
+        nc.vector.tensor_copy(out=c_cols[:], in_=vec_flip[:, PACK, GROUPS : GROUPS + J_TILES])
+        nc.vector.quantize_mx(out=x_codes[:].bitcast(FP8X4), scales=x_planes[:], in_=x_grouped[:])
+
+        def spread_s(pair):
+            s_bank = psum_flip.tile([P, 2, PACK, P], BF16, tag="flip")
+            for a in range(2):
+                for t in range(PACK):
+                    nc.tensor.matmul(
+                        out=s_bank[:, a, t, :],
+                        lhsT=s_cols[:, 2 * pair + a, t : t + 1].to_broadcast([P, P]),
+                        rhs=ident_bf16[:],
+                        start=True,
+                        stop=True,
+                    )
+            nc.scalar.copy(out=s_all[:, 2 * pair : 2 * pair + 2, :, :], in_=s_bank[:])
+
+        def distances(batch):
+            for g in range(GROUPS):
+                if batch[0] == 0 and g + 2 < GROUPS // 2:
+                    spread_s(g + 2)
+                cols = slice(g * K_PASS, (g + 1) * K_PASS)
+                for jt in batch:
+                    cross = psum_cross.tile([P, K_PASS], F32)
+                    nc.tensor.matmul_mx(
+                        out=cross[:],
+                        lhsT=x_codes[:, jt * P : (jt + 1) * P].bitcast(FP8X4),
+                        lhsT_scale=x_planes[:, jt * P : (jt + 1) * P],
+                        rhs=sm_codes[:, cols].bitcast(FP8X4),
+                        rhs_scale=sm_planes[:, cols],
+                        start=True,
+                        stop=True,
+                    )
+                    nc.vector.scalar_tensor_tensor(
+                        out=k_tiles[jt][:, cols].rearrange("p (t n) -> p t n", t=PACK),
+                        in0=cross[:].rearrange("p (n t) -> p t n", t=PACK),
+                        scalar=-2.0,
+                        in1=s_all[:, g, :, :],
+                        op0=ALU.mult,
+                        op1=ALU.add,
+                    )
+                done = (g + 1) * K_PASS
+                if done % CLAMP_COLS == 0:
+                    for jt in batch:
+                        piece = k_tiles[jt][:, done - CLAMP_COLS : done]
+                        nc.gpsimd.tensor_scalar(
+                            out=piece,
+                            in0=piece,
+                            scalar1=c_cols[:, jt : jt + 1],
+                            scalar2=SQRT_FLOOR,
+                            op0=ALU.add,
+                            op1=ALU.max,
+                        )
+                        nc.scalar.activation(out=piece, in_=piece, func=ACT.Sqrt)
+
+        def kernel_values(jt):
+            for e in range(NTR // EXP_COLS):
+                piece = k_tiles[jt][:, e * EXP_COLS : (e + 1) * EXP_COLS]
+                nc.scalar.activation(
+                    out=piece,
+                    in_=piece,
+                    func=ACT.Exp,
+                    scale=-1.0 / GAMMA,
+                    accum_out=k_sums[:, jt, e : e + 1],
+                )
+
+        def smooth(jt):
+            total = work.tile([P, 1], F32)
+            nc.vector.reduce_sum(out=total[:], in_=k_sums[:, jt, :], axis=mybir.AxisListType.X)
+            inverse = work.tile([P, 1], F32)
+            nc.vector.reciprocal(out=inverse[:], in_=total[:])
+            inverse_wide = work.tile([P, P], F32)
+            nc.vector.tensor_copy(out=inverse_wide[:], in_=inverse[:, 0:1].to_broadcast([P, P]))
+            inverse_flip = psum_one.tile([P, P], F32, tag="small")
+            nc.tensor.transpose(inverse_flip[:], inverse_wide[:], ident_f32[:])
+            inverse_row = work.tile([P, P], F32)
+            nc.vector.tensor_copy(out=inverse_row[:], in_=inverse_flip[:])
+
+            quads = {}
+
+            def quantise(q):
+                w_grouped, w_codes, w_planes = quads[q]
+                nc.vector.quantize_mx(
+                    out=w_codes[:].rearrange("p a j -> p (a j)").bitcast(FP8X4),
+                    scales=w_planes[:].rearrange("p a j -> p (a j)"),
+                    in_=w_grouped[:].rearrange("p a j t -> p (a j t)"),
+                )
+
+            def multiply(q):
+                w_grouped, w_codes, w_planes = quads[q]
+                for a in range(QUAD):
+                    g = QUAD * q + a
+                    nc.tensor.matmul_mx(
+                        out=out_acc[:, jt, :],
+                        lhsT=w_codes[:, a, :].bitcast(FP8X4),
+                        lhsT_scale=w_planes[:, a, :],
+                        rhs=y_codes[:, g, :].bitcast(FP8X4),
+                        rhs_scale=y_planes[:, g, :],
+                        start=(g == 0),
+                        stop=(g == GROUPS - 1),
+                    )
+
+            for g in range(GROUPS):
+                q, a = divmod(g, QUAD)
+                if a == 0:
+                    w_grouped = work.tile([P, QUAD, P, PACK], BF16, align_bytes=64, bufs=3)
+                    w_codes = work.tile([P, QUAD, P], U32, align_bytes=64, bufs=3)
+                    w_planes = work.tile([P, QUAD, P], U8, align_bytes=64, bufs=3)
+                    quads[q] = (w_grouped, w_codes, w_planes)
+                k_flip = psum_flip.tile([P, PACK, P], F32, tag="flip")
+                for t in range(PACK):
+                    first = (PACK * g + t) * P
+                    nc.tensor.transpose(k_flip[:, t, :], k_tiles[jt][:, first : first + P], ident_f32[:])
+                nc.vector.tensor_tensor(
+                    out=quads[q][0][:, a, :, :],
+                    in0=k_flip[:].rearrange("p t j -> p j t"),
+                    in1=inverse_row[:].unsqueeze(2).to_broadcast([P, P, PACK]),
+                    op=ALU.mult,
+                )
+                if a == 0 and q > 0:
+                    quantise(q - 1)
+                if a == QUAD - 1 and q > 0:
+                    multiply(q - 1)
+            quantise(GROUPS // QUAD - 1)
+            multiply(GROUPS // QUAD - 1)
+            out_sb = work.tile([P, C], F32)
+            nc.vector.tensor_copy(out=out_sb[:], in_=out_acc[:, jt, :])
+            nc.sync.dma_start(out=out[jt * P : (jt + 1) * P, :], in_=out_sb[:])
+
+        spread_s(0)
+        spread_s(1)
+        distances((0, 1))
+        kernel_values(0)
+        kernel_values(1)
+        distances((2, 3))
+        smooth(0)
+        smooth(1)
+        kernel_values(2)
+        kernel_values(3)
+        smooth(2)
+        smooth(3)

@@ -138,6 +138,19 @@ def tile_rbfnet_pb_t_kernel(
                     )
             nc.scalar.copy(out=s_all[:, 2 * pair : 2 * pair + 2, :, :], in_=s_bank[:])
 
+        def clamp_and_root(batch, done):
+            for jt in batch:
+                piece = k_tiles[jt][:, done - CLAMP_COLS : done]
+                nc.vector.tensor_scalar(
+                    out=piece,
+                    in0=piece,
+                    scalar1=c_cols[:, jt : jt + 1],
+                    scalar2=SQRT_FLOOR,
+                    op0=ALU.add,
+                    op1=ALU.max,
+                )
+                nc.scalar.activation(out=piece, in_=piece, func=ACT.Sqrt)
+
         def distances(batch):
             for g in range(GROUPS):
                 if batch[0] == 0 and g + 2 < GROUPS // 2:
@@ -162,19 +175,9 @@ def tile_rbfnet_pb_t_kernel(
                         op0=ALU.mult,
                         op1=ALU.add,
                     )
-                done = (g + 1) * K_PASS
-                if done % CLAMP_COLS == 0:
-                    for jt in batch:
-                        piece = k_tiles[jt][:, done - CLAMP_COLS : done]
-                        nc.gpsimd.tensor_scalar(
-                            out=piece,
-                            in0=piece,
-                            scalar1=c_cols[:, jt : jt + 1],
-                            scalar2=SQRT_FLOOR,
-                            op0=ALU.add,
-                            op1=ALU.max,
-                        )
-                        nc.scalar.activation(out=piece, in_=piece, func=ACT.Sqrt)
+                if g > 0 and (g * K_PASS) % CLAMP_COLS == 0:
+                    clamp_and_root(batch, g * K_PASS)
+            clamp_and_root(batch, NTR)
 
         def kernel_values(jt):
             for e in range(NTR // EXP_COLS):

@@ -19,7 +19,9 @@ NTR, NTE, D, C = 8192, 512, 512, 128
 GAMMA = 10.0
 J_TILES = NTE // P
 GROUPS = NTR // K_PASS
-QUAD = 4
+PAIR = 2
+AHEAD = 2
+WIDE = 128
 CLAMP_COLS = 1024
 EXP_COLS = 2048
 WORD_LOAD_COLS = 1024
@@ -35,8 +37,7 @@ def tile_rbfnet_pb_t_kernel(
     with ExitStack() as ctx:
         keep = ctx.enter_context(tc.tile_pool(name="keep", bufs=1))
         work = ctx.enter_context(tc.tile_pool(name="work", bufs=2))
-        psum_cross = ctx.enter_context(tc.psum_pool(name="psum_cross", bufs=3))
-        psum_flip = ctx.enter_context(tc.psum_pool(name="psum_flip", bufs=3))
+        psum_ring = ctx.enter_context(tc.psum_pool(name="psum_ring", bufs=6))
         psum_one = ctx.enter_context(tc.psum_pool(name="psum_one", bufs=1))
         ctx.enter_context(tc.manual_schedule())
 
@@ -46,8 +47,9 @@ def tile_rbfnet_pb_t_kernel(
         x_planes = keep.tile([P, NTE], U8, align_bytes=64)
         sm_codes = keep.tile([P, NTR], U32, align_bytes=64)
         sm_planes = keep.tile([P, NTR], U8, align_bytes=64)
-        y_codes = keep.tile([P, GROUPS, C], U32, align_bytes=64)
-        y_planes = keep.tile([P, GROUPS, C], U8, align_bytes=64)
+        y_groups = GROUPS + WIDE // C - 1
+        y_codes = keep.tile([P, y_groups, C], U32, align_bytes=64)
+        y_planes = keep.tile([P, y_groups, C], U8, align_bytes=64)
         vec_rows = keep.tile([P, K_PASS], BF16)
         s_cols = keep.tile([P, GROUPS, PACK], BF16)
         c_cols = keep.tile([P, J_TILES], F32)
@@ -57,7 +59,6 @@ def tile_rbfnet_pb_t_kernel(
         warm = keep.tile([P, 2], F32)
         k_sums = keep.tile([P, J_TILES, NTR // EXP_COLS], F32)
         k_tiles = [keep.tile([P, NTR], F32, name="k_tile%d" % jt) for jt in range(J_TILES)]
-        out_acc = psum_one.tile([P, J_TILES, C], F32)
 
         nc.vector.memset(sm_planes[:].bitcast(I32), 0)
         nc.vector.memset(vec_rows[:], 0.0)
@@ -90,19 +91,19 @@ def tile_rbfnet_pb_t_kernel(
             )
         for quadrant in range(4):
             nc.sync.dma_start(
-                out=y_planes[32 * quadrant : 32 * quadrant + 4, :, :].bitcast(I32),
+                out=y_planes[32 * quadrant : 32 * quadrant + 4, 0:GROUPS, :].bitcast(I32),
                 in_=y_train_scales[:, 4 * quadrant : 4 * quadrant + 4, :]
                 .rearrange("g r n -> r g n")
                 .bitcast(I32),
             )
         nc.sync.dma_start(
-            out=y_codes[:].bitcast(I32),
+            out=y_codes[:, 0:GROUPS, :].bitcast(I32),
             in_=y_train_words.rearrange("g p n t -> p g (n t)").bitcast(I32),
         )
 
         x_grouped_words = x_grouped[:].bitcast(F32).rearrange("p (a j u) -> p a j u", a=J_TILES, u=2)
         for pair in range(J_TILES // 2):
-            x_flip = psum_flip.tile([P, 2, 2, P], F32, tag="flip")
+            x_flip = psum_ring.tile([P, 2, 2, P], F32, tag="ring")
             for a in range(2):
                 for u in range(2):
                     nc.tensor.transpose(
@@ -126,7 +127,7 @@ def tile_rbfnet_pb_t_kernel(
         nc.vector.quantize_mx(out=x_codes[:].bitcast(FP8X4), scales=x_planes[:], in_=x_grouped[:])
 
         def spread_s(pair):
-            s_bank = psum_flip.tile([P, 2, PACK, P], BF16, tag="flip")
+            s_bank = psum_ring.tile([P, 2, PACK, P], BF16, tag="ring")
             for a in range(2):
                 for t in range(PACK):
                     nc.tensor.matmul(
@@ -157,7 +158,7 @@ def tile_rbfnet_pb_t_kernel(
                     spread_s(g + 2)
                 cols = slice(g * K_PASS, (g + 1) * K_PASS)
                 for jt in batch:
-                    cross = psum_cross.tile([P, K_PASS], F32)
+                    cross = psum_ring.tile([P, K_PASS], F32, tag="ring")
                     nc.tensor.matmul_mx(
                         out=cross[:],
                         lhsT=x_codes[:, jt * P : (jt + 1) * P].bitcast(FP8X4),
@@ -202,55 +203,63 @@ def tile_rbfnet_pb_t_kernel(
             inverse_row = work.tile([P, P], F32)
             nc.vector.tensor_copy(out=inverse_row[:], in_=inverse_flip[:])
 
-            quads = {}
+            out_acc = psum_one.tile([P, WIDE], F32)
+            flips = {}
+            pairs = {}
 
-            def quantise(q):
-                w_grouped, w_codes, w_planes = quads[q]
+            def flip(g):
+                k_flip = psum_ring.tile([P, PACK, P], F32, tag="ring")
+                for t in range(PACK):
+                    first = (PACK * g + t) * P
+                    nc.tensor.transpose(k_flip[:, t, :], k_tiles[jt][:, first : first + P], ident_f32[:])
+                flips[g] = k_flip
+
+            def quantise(h):
+                w_grouped, w_codes, w_planes = pairs[h]
                 nc.vector.quantize_mx(
                     out=w_codes[:].rearrange("p a j -> p (a j)").bitcast(FP8X4),
                     scales=w_planes[:].rearrange("p a j -> p (a j)"),
                     in_=w_grouped[:].rearrange("p a j t -> p (a j t)"),
                 )
 
-            def multiply(q):
-                w_grouped, w_codes, w_planes = quads[q]
-                for a in range(QUAD):
-                    g = QUAD * q + a
+            def multiply(h):
+                w_grouped, w_codes, w_planes = pairs[h]
+                for a in range(PAIR):
+                    g = PAIR * h + a
                     nc.tensor.matmul_mx(
-                        out=out_acc[:, jt, :],
+                        out=out_acc[:],
                         lhsT=w_codes[:, a, :].bitcast(FP8X4),
                         lhsT_scale=w_planes[:, a, :],
-                        rhs=y_codes[:, g, :].bitcast(FP8X4),
-                        rhs_scale=y_planes[:, g, :],
+                        rhs=y_codes[:, g : g + WIDE // C, :].rearrange("p g c -> p (g c)").bitcast(FP8X4),
+                        rhs_scale=y_planes[:, g : g + WIDE // C, :].rearrange("p g c -> p (g c)"),
                         start=(g == 0),
                         stop=(g == GROUPS - 1),
                     )
 
+            for g in range(AHEAD):
+                flip(g)
             for g in range(GROUPS):
-                q, a = divmod(g, QUAD)
+                h, a = divmod(g, PAIR)
+                if g + AHEAD < GROUPS:
+                    flip(g + AHEAD)
                 if a == 0:
-                    w_grouped = work.tile([P, QUAD, P, PACK], BF16, align_bytes=64, bufs=3)
-                    w_codes = work.tile([P, QUAD, P], U32, align_bytes=64, bufs=3)
-                    w_planes = work.tile([P, QUAD, P], U8, align_bytes=64, bufs=3)
-                    quads[q] = (w_grouped, w_codes, w_planes)
-                k_flip = psum_flip.tile([P, PACK, P], F32, tag="flip")
-                for t in range(PACK):
-                    first = (PACK * g + t) * P
-                    nc.tensor.transpose(k_flip[:, t, :], k_tiles[jt][:, first : first + P], ident_f32[:])
+                    w_grouped = work.tile([P, PAIR, P, PACK], BF16, align_bytes=64, bufs=3)
+                    w_codes = work.tile([P, PAIR, P], U32, align_bytes=64, bufs=3)
+                    w_planes = work.tile([P, PAIR, P], U8, align_bytes=64, bufs=3)
+                    pairs[h] = (w_grouped, w_codes, w_planes)
                 nc.vector.tensor_tensor(
-                    out=quads[q][0][:, a, :, :],
-                    in0=k_flip[:].rearrange("p t j -> p j t"),
+                    out=pairs[h][0][:, a, :, :],
+                    in0=flips[g][:].rearrange("p t j -> p j t"),
                     in1=inverse_row[:].unsqueeze(2).to_broadcast([P, P, PACK]),
                     op=ALU.mult,
                 )
-                if a == 0 and q > 0:
-                    quantise(q - 1)
-                if a == QUAD - 1 and q > 0:
-                    multiply(q - 1)
-            quantise(GROUPS // QUAD - 1)
-            multiply(GROUPS // QUAD - 1)
+                if a == 0 and h > 0:
+                    quantise(h - 1)
+                    multiply(h - 1)
+            quantise(GROUPS // PAIR - 1)
+            multiply(GROUPS // PAIR - 1)
             out_sb = work.tile([P, C], F32)
-            nc.vector.tensor_copy(out=out_sb[:], in_=out_acc[:, jt, :])
+            nc.vector.tensor_copy(out=out_sb[:], in_=out_acc[:, 0:C])
             nc.sync.dma_start(out=out[jt * P : (jt + 1) * P, :], in_=out_sb[:])
 
         spread_s(0)

@@ -21,7 +21,7 @@ J_TILES = NTE // P
 GROUPS = NTR // K_PASS
 PAIR = 2
 AHEAD = 2
-WIDE = 128
+WIDE = 512
 CLAMP_COLS = 1024
 EXP_COLS = 2048
 WORD_LOAD_COLS = 1024
@@ -64,6 +64,7 @@ def tile_rbfnet_pb_t_kernel(
         nc.vector.memset(vec_rows[:], 0.0)
         nc.vector.memset(warm[:], 1.0)
         nc.vector.memset(y_planes[:].rearrange("p g c -> p (g c)").bitcast(I32), 0)
+        nc.vector.memset(y_codes[:, GROUPS:y_groups, :].rearrange("p g c -> p (g c)").bitcast(I32), 0)
         make_identity(nc, ident_f32[:])
         make_identity(nc, ident_bf16[:])
         nc.scalar.activation(out=warm[:, 1:2], in_=warm[:, 0:1], func=ACT.Sqrt)

@@ -20,11 +20,15 @@ GAMMA = 10.0
 J_TILES = NTE // P
 GROUPS = NTR // K_PASS
 PAIR = 2
-AHEAD = 2
-WIDE = 512
+UNIT_COLS = PAIR * K_PASS
+TILE_UNITS = NTR // UNIT_COLS
+UNITS = J_TILES * TILE_UNITS
+LEAD = 2
+HELP_FROM = 21
 CLAMP_COLS = 1024
 EXP_COLS = 2048
 WORD_LOAD_COLS = 1024
+PLANE_COLS = NTR // 4
 SQRT_FLOOR = 2.0 ** -100
 
 FLOPS = 2 * NTR * NTE * D + 2 * NTE * NTR * C
@@ -38,7 +42,7 @@ def tile_rbfnet_pb_t_kernel(
         keep = ctx.enter_context(tc.tile_pool(name="keep", bufs=1))
         work = ctx.enter_context(tc.tile_pool(name="work", bufs=2))
         psum_ring = ctx.enter_context(tc.psum_pool(name="psum_ring", bufs=6))
-        psum_one = ctx.enter_context(tc.psum_pool(name="psum_one", bufs=1))
+        psum_out = ctx.enter_context(tc.psum_pool(name="psum_out", bufs=2))
         ctx.enter_context(tc.manual_schedule())
 
         x_sb = keep.tile([P, J_TILES, D], BF16)
@@ -46,10 +50,9 @@ def tile_rbfnet_pb_t_kernel(
         x_codes = keep.tile([P, NTE], U32, align_bytes=64)
         x_planes = keep.tile([P, NTE], U8, align_bytes=64)
         sm_codes = keep.tile([P, NTR], U32, align_bytes=64)
-        sm_planes = keep.tile([P, NTR], U8, align_bytes=64)
-        y_groups = GROUPS + WIDE // C - 1
-        y_codes = keep.tile([P, y_groups, C], U32, align_bytes=64)
-        y_planes = keep.tile([P, y_groups, C], U8, align_bytes=64)
+        sm_planes = keep.tile([P, PLANE_COLS], U8, align_bytes=64)
+        y_codes = keep.tile([P, GROUPS, C], U32, align_bytes=64)
+        y_planes = keep.tile([P, GROUPS, C], U8, align_bytes=64)
         vec_rows = keep.tile([P, K_PASS], BF16)
         s_cols = keep.tile([P, GROUPS, PACK], BF16)
         c_cols = keep.tile([P, J_TILES], F32)
@@ -60,30 +63,27 @@ def tile_rbfnet_pb_t_kernel(
         k_sums = keep.tile([P, J_TILES, NTR // EXP_COLS], F32)
         k_tiles = [keep.tile([P, NTR], F32, name="k_tile%d" % jt) for jt in range(J_TILES)]
 
-        nc.vector.memset(sm_planes[:].bitcast(I32), 0)
         nc.vector.memset(vec_rows[:], 0.0)
+        nc.vector.memset(sm_planes[:].bitcast(I32), 0)
         nc.vector.memset(warm[:], 1.0)
         nc.vector.memset(y_planes[:].rearrange("p g c -> p (g c)").bitcast(I32), 0)
-        nc.vector.memset(y_codes[:, GROUPS:y_groups, :].rearrange("p g c -> p (g c)").bitcast(I32), 0)
-        make_identity(nc, ident_f32[:])
         make_identity(nc, ident_bf16[:])
+        make_identity(nc, ident_f32[:])
         nc.scalar.activation(out=warm[:, 1:2], in_=warm[:, 0:1], func=ACT.Sqrt)
 
-        nc.sync.dma_start(out=x_sb[:], in_=x_test.rearrange("(a p) k -> p a k", p=P))
         nc.sync.dma_start(out=vec_rows[0:GROUPS, :], in_=s_norm2.rearrange("(g n) -> g n", g=GROUPS))
         nc.sync.dma_start(
             out=vec_rows[GROUPS : GROUPS + J_TILES, 0:P],
             in_=c_norm2.rearrange("(a n) -> a n", a=J_TILES),
         )
-        sm_scale_rows = sM_scales.rearrange("o q n -> (o q) n")
-        for half in range(2):
-            cols = slice(half * (NTR // 2), (half + 1) * (NTR // 2))
-            for b in range(2):
-                for r in range(4):
-                    nc.sync.dma_start(
-                        out=sm_planes[32 * b + r : P : 64, cols].bitcast(I32),
-                        in_=sm_scale_rows[4 * b + r : 16 : 8, cols].bitcast(I32),
-                    )
+        nc.sync.dma_start(out=x_sb[:], in_=x_test.rearrange("(a p) k -> p a k", p=P))
+        for quadrant in range(4):
+            nc.sync.dma_start(
+                out=sm_planes[32 * quadrant : 32 * quadrant + 16, :].bitcast(I32),
+                in_=sM_scales[0, 4 * quadrant : 4 * quadrant + 4, :]
+                .rearrange("r (v n) -> v r n", v=4)
+                .bitcast(I32),
+            )
         sm_word_bytes = sM_words.rearrange("o p n t -> (o p) (n t)")
         for first in range(0, NTR, WORD_LOAD_COLS):
             nc.sync.dma_start(
@@ -92,16 +92,24 @@ def tile_rbfnet_pb_t_kernel(
             )
         for quadrant in range(4):
             nc.sync.dma_start(
-                out=y_planes[32 * quadrant : 32 * quadrant + 4, 0:GROUPS, :].bitcast(I32),
+                out=y_planes[32 * quadrant : 32 * quadrant + 4, :, :].bitcast(I32),
                 in_=y_train_scales[:, 4 * quadrant : 4 * quadrant + 4, :]
                 .rearrange("g r n -> r g n")
                 .bitcast(I32),
             )
         nc.sync.dma_start(
-            out=y_codes[:, 0:GROUPS, :].bitcast(I32),
+            out=y_codes[:].bitcast(I32),
             in_=y_train_words.rearrange("g p n t -> p g (n t)").bitcast(I32),
         )
 
+        vec_flip = psum_ring.tile([P, PACK + 1, P], BF16, tag="ring")
+        for t in range(PACK):
+            nc.tensor.transpose(vec_flip[:, t, :], vec_rows[:, t:K_PASS:PACK], ident_bf16[:])
+        nc.tensor.transpose(vec_flip[:, PACK, :], vec_rows[:, 0:P], ident_bf16[:])
+        nc.vector.tensor_copy(
+            out=s_cols[:], in_=vec_flip[:, 0:PACK, 0:GROUPS].rearrange("p t g -> p g t")
+        )
+        nc.vector.tensor_copy(out=c_cols[:], in_=vec_flip[:, PACK, GROUPS : GROUPS + J_TILES])
         x_grouped_words = x_grouped[:].bitcast(F32).rearrange("p (a j u) -> p a j u", a=J_TILES, u=2)
         for pair in range(J_TILES // 2):
             x_flip = psum_ring.tile([P, 2, 2, P], F32, tag="ring")
@@ -117,14 +125,6 @@ def tile_rbfnet_pb_t_kernel(
                 in_=x_flip[:].rearrange("p a u j -> p a j u"),
             )
 
-        vec_flip = psum_one.tile([P, PACK + 1, P], BF16, tag="small")
-        for t in range(PACK):
-            nc.tensor.transpose(vec_flip[:, t, :], vec_rows[:, t:K_PASS:PACK], ident_bf16[:])
-        nc.tensor.transpose(vec_flip[:, PACK, :], vec_rows[:, 0:P], ident_bf16[:])
-        nc.vector.tensor_copy(
-            out=s_cols[:], in_=vec_flip[:, 0:PACK, 0:GROUPS].rearrange("p t g -> p g t")
-        )
-        nc.vector.tensor_copy(out=c_cols[:], in_=vec_flip[:, PACK, GROUPS : GROUPS + J_TILES])
         nc.vector.quantize_mx(out=x_codes[:].bitcast(FP8X4), scales=x_planes[:], in_=x_grouped[:])
 
         def spread_s(pair):
@@ -158,6 +158,8 @@ def tile_rbfnet_pb_t_kernel(
                 if batch[0] == 0 and g + 2 < GROUPS // 2:
                     spread_s(g + 2)
                 cols = slice(g * K_PASS, (g + 1) * K_PASS)
+                quarter, first = divmod(g * K_PASS, PLANE_COLS)
+                plane_cols = slice(first, first + K_PASS)
                 for jt in batch:
                     cross = psum_ring.tile([P, K_PASS], F32, tag="ring")
                     nc.tensor.matmul_mx(
@@ -165,7 +167,7 @@ def tile_rbfnet_pb_t_kernel(
                         lhsT=x_codes[:, jt * P : (jt + 1) * P].bitcast(FP8X4),
                         lhsT_scale=x_planes[:, jt * P : (jt + 1) * P],
                         rhs=sm_codes[:, cols].bitcast(FP8X4),
-                        rhs_scale=sm_planes[:, cols],
+                        rhs_scale=sm_planes[PACK * quarter : P, plane_cols],
                         start=True,
                         stop=True,
                     )
@@ -192,75 +194,83 @@ def tile_rbfnet_pb_t_kernel(
                     accum_out=k_sums[:, jt, e : e + 1],
                 )
 
-        def smooth(jt):
+        inverses = {}
+        rows = {}
+        flips = {}
+        packs = {}
+        sums = {}
+
+        def scalar_helps(u):
+            return u >= HELP_FROM and u % 2 == 1
+
+        def invert_sum(jt):
             total = work.tile([P, 1], F32)
             nc.vector.reduce_sum(out=total[:], in_=k_sums[:, jt, :], axis=mybir.AxisListType.X)
             inverse = work.tile([P, 1], F32)
             nc.vector.reciprocal(out=inverse[:], in_=total[:])
-            inverse_wide = work.tile([P, P], F32)
-            nc.vector.tensor_copy(out=inverse_wide[:], in_=inverse[:, 0:1].to_broadcast([P, P]))
-            inverse_flip = psum_one.tile([P, P], F32, tag="small")
-            nc.tensor.transpose(inverse_flip[:], inverse_wide[:], ident_f32[:])
-            inverse_row = work.tile([P, P], F32)
-            nc.vector.tensor_copy(out=inverse_row[:], in_=inverse_flip[:])
+            inverses[jt] = inverse
 
-            out_acc = psum_one.tile([P, WIDE], F32)
-            flips = {}
-            pairs = {}
+        def normalise(u):
+            jt, h = divmod(u, TILE_UNITS)
+            piece = k_tiles[jt][:, h * UNIT_COLS : (h + 1) * UNIT_COLS]
+            w_rows = work.tile([P, UNIT_COLS], BF16, bufs=4)
+            if scalar_helps(u):
+                nc.scalar.activation(out=w_rows[:], in_=piece, func=ACT.Copy, scale=inverses[jt][:, 0:1])
+            else:
+                nc.gpsimd.tensor_scalar(
+                    out=w_rows[:],
+                    in0=piece,
+                    scalar1=inverses[jt][:, 0:1],
+                    scalar2=0.0,
+                    op0=ALU.mult,
+                    op1=ALU.add,
+                )
+            rows[u] = w_rows
 
-            def flip(g):
-                k_flip = psum_ring.tile([P, PACK, P], F32, tag="ring")
+        def flip(u):
+            w_flip = psum_ring.tile([P, PAIR, PACK, P], BF16, tag="ring")
+            for a in range(PAIR):
                 for t in range(PACK):
-                    first = (PACK * g + t) * P
-                    nc.tensor.transpose(k_flip[:, t, :], k_tiles[jt][:, first : first + P], ident_f32[:])
-                flips[g] = k_flip
+                    first = (PACK * a + t) * P
+                    nc.tensor.transpose(w_flip[:, a, t, :], rows[u][:, first : first + P], ident_bf16[:])
+            flips[u] = w_flip
 
-            def quantise(h):
-                w_grouped, w_codes, w_planes = pairs[h]
-                nc.vector.quantize_mx(
-                    out=w_codes[:].rearrange("p a j -> p (a j)").bitcast(FP8X4),
-                    scales=w_planes[:].rearrange("p a j -> p (a j)"),
-                    in_=w_grouped[:].rearrange("p a j t -> p (a j t)"),
+        def empty(u):
+            w_grouped = work.tile([P, PAIR, P, PACK], BF16, align_bytes=64, bufs=4)
+            source = flips[u][:].rearrange("p a t j -> p a j t")
+            if scalar_helps(u):
+                nc.scalar.copy(out=w_grouped[:], in_=source)
+            else:
+                nc.vector.tensor_copy(out=w_grouped[:], in_=source)
+            packs[u] = w_grouped
+
+        def quantise_and_multiply(u):
+            jt, h = divmod(u, TILE_UNITS)
+            w_codes = work.tile([P, PAIR, P], U32, align_bytes=64, bufs=3)
+            w_planes = work.tile([P, PAIR, P], U8, align_bytes=64, bufs=3)
+            nc.vector.quantize_mx(
+                out=w_codes[:].rearrange("p a j -> p (a j)").bitcast(FP8X4),
+                scales=w_planes[:].rearrange("p a j -> p (a j)"),
+                in_=packs[u][:].rearrange("p a j t -> p (a j t)"),
+            )
+            if h == 0:
+                out_acc = psum_out.tile([P, C], F32)
+                sums[jt] = out_acc
+            for a in range(PAIR):
+                g = PAIR * h + a
+                nc.tensor.matmul_mx(
+                    out=sums[jt][:],
+                    lhsT=w_codes[:, a, :].bitcast(FP8X4),
+                    lhsT_scale=w_planes[:, a, :],
+                    rhs=y_codes[:, g, :].bitcast(FP8X4),
+                    rhs_scale=y_planes[:, g, :],
+                    start=(g == 0),
+                    stop=(g == GROUPS - 1),
                 )
 
-            def multiply(h):
-                w_grouped, w_codes, w_planes = pairs[h]
-                for a in range(PAIR):
-                    g = PAIR * h + a
-                    nc.tensor.matmul_mx(
-                        out=out_acc[:],
-                        lhsT=w_codes[:, a, :].bitcast(FP8X4),
-                        lhsT_scale=w_planes[:, a, :],
-                        rhs=y_codes[:, g : g + WIDE // C, :].rearrange("p g c -> p (g c)").bitcast(FP8X4),
-                        rhs_scale=y_planes[:, g : g + WIDE // C, :].rearrange("p g c -> p (g c)"),
-                        start=(g == 0),
-                        stop=(g == GROUPS - 1),
-                    )
-
-            for g in range(AHEAD):
-                flip(g)
-            for g in range(GROUPS):
-                h, a = divmod(g, PAIR)
-                if g + AHEAD < GROUPS:
-                    flip(g + AHEAD)
-                if a == 0:
-                    w_grouped = work.tile([P, PAIR, P, PACK], BF16, align_bytes=64, bufs=3)
-                    w_codes = work.tile([P, PAIR, P], U32, align_bytes=64, bufs=3)
-                    w_planes = work.tile([P, PAIR, P], U8, align_bytes=64, bufs=3)
-                    pairs[h] = (w_grouped, w_codes, w_planes)
-                nc.vector.tensor_tensor(
-                    out=pairs[h][0][:, a, :, :],
-                    in0=flips[g][:].rearrange("p t j -> p j t"),
-                    in1=inverse_row[:].unsqueeze(2).to_broadcast([P, P, PACK]),
-                    op=ALU.mult,
-                )
-                if a == 0 and h > 0:
-                    quantise(h - 1)
-                    multiply(h - 1)
-            quantise(GROUPS // PAIR - 1)
-            multiply(GROUPS // PAIR - 1)
+        def store(jt):
             out_sb = work.tile([P, C], F32)
-            nc.vector.tensor_copy(out=out_sb[:], in_=out_acc[:, 0:C])
+            nc.vector.tensor_copy(out=out_sb[:], in_=sums[jt][:])
             nc.sync.dma_start(out=out[jt * P : (jt + 1) * P, :], in_=out_sb[:])
 
         spread_s(0)
@@ -269,9 +279,17 @@ def tile_rbfnet_pb_t_kernel(
         kernel_values(0)
         kernel_values(1)
         distances((2, 3))
-        smooth(0)
-        smooth(1)
         kernel_values(2)
         kernel_values(3)
-        smooth(2)
-        smooth(3)
+        for s in range(UNITS + LEAD + 2):
+            if s < UNITS:
+                if s % TILE_UNITS == 0:
+                    invert_sum(s // TILE_UNITS)
+                normalise(s)
+                flip(s)
+            if 0 <= s - LEAD < UNITS:
+                empty(s - LEAD)
+            if 0 <= s - LEAD - 1 < UNITS:
+                quantise_and_multiply(s - LEAD - 1)
+            if s - LEAD - 2 >= 0 and (s - LEAD - 2) % TILE_UNITS == TILE_UNITS - 1:
+                store((s - LEAD - 2) // TILE_UNITS)

@@ -23,7 +23,8 @@ PAIR = 2
 UNIT_COLS = PAIR * K_PASS
 TILE_UNITS = NTR // UNIT_COLS
 UNITS = J_TILES * TILE_UNITS
-LEAD = 2
+LEAD = 3
+BURST = 4
 HELP_FROM = 21
 CLAMP_COLS = 1024
 EXP_COLS = 2048
@@ -198,6 +199,7 @@ def tile_rbfnet_pb_t_kernel(
         rows = {}
         flips = {}
         packs = {}
+        codes = {}
         sums = {}
 
         def scalar_helps(u):
@@ -244,15 +246,19 @@ def tile_rbfnet_pb_t_kernel(
                 nc.vector.tensor_copy(out=w_grouped[:], in_=source)
             packs[u] = w_grouped
 
-        def quantise_and_multiply(u):
-            jt, h = divmod(u, TILE_UNITS)
-            w_codes = work.tile([P, PAIR, P], U32, align_bytes=64, bufs=3)
-            w_planes = work.tile([P, PAIR, P], U8, align_bytes=64, bufs=3)
+        def quantise(u):
+            w_codes = work.tile([P, PAIR, P], U32, align_bytes=64, bufs=2 * BURST)
+            w_planes = work.tile([P, PAIR, P], U8, align_bytes=64, bufs=2 * BURST)
             nc.vector.quantize_mx(
                 out=w_codes[:].rearrange("p a j -> p (a j)").bitcast(FP8X4),
                 scales=w_planes[:].rearrange("p a j -> p (a j)"),
                 in_=packs[u][:].rearrange("p a j t -> p (a j t)"),
             )
+            codes[u] = (w_codes, w_planes)
+
+        def multiply(u):
+            jt, h = divmod(u, TILE_UNITS)
+            w_codes, w_planes = codes[u]
             if h == 0:
                 out_acc = psum_out.tile([P, C], F32)
                 sums[jt] = out_acc
@@ -289,7 +295,11 @@ def tile_rbfnet_pb_t_kernel(
                 flip(s)
             if 0 <= s - LEAD < UNITS:
                 empty(s - LEAD)
-            if 0 <= s - LEAD - 1 < UNITS:
-                quantise_and_multiply(s - LEAD - 1)
-            if s - LEAD - 2 >= 0 and (s - LEAD - 2) % TILE_UNITS == TILE_UNITS - 1:
-                store((s - LEAD - 2) // TILE_UNITS)
+            ready = s - LEAD - 1
+            if 0 <= ready < UNITS:
+                quantise(ready)
+                if ready % BURST == BURST - 1:
+                    for u in range(ready - BURST + 1, ready + 1):
+                        multiply(u)
+            if ready - 1 >= 0 and (ready - 1) % TILE_UNITS == TILE_UNITS - 1:
+                store((ready - 1) // TILE_UNITS)

@@ -23,7 +23,7 @@ PAIR = 2
 UNIT_COLS = PAIR * K_PASS
 TILE_UNITS = NTR // UNIT_COLS
 UNITS = J_TILES * TILE_UNITS
-LEAD = 3
+LEAD = 2
 BURST = 4
 HELP_FROM = 21
 CLAMP_COLS = 1024
@@ -196,7 +196,6 @@ def tile_rbfnet_pb_t_kernel(
                 )
 
         inverses = {}
-        rows = {}
         flips = {}
         packs = {}
         codes = {}
@@ -215,35 +214,37 @@ def tile_rbfnet_pb_t_kernel(
         def normalise(u):
             jt, h = divmod(u, TILE_UNITS)
             piece = k_tiles[jt][:, h * UNIT_COLS : (h + 1) * UNIT_COLS]
-            w_rows = work.tile([P, UNIT_COLS], BF16, bufs=4)
             if scalar_helps(u):
-                nc.scalar.activation(out=w_rows[:], in_=piece, func=ACT.Copy, scale=inverses[jt][:, 0:1])
+                nc.scalar.activation(out=piece, in_=piece, func=ACT.Copy, scale=inverses[jt][:, 0:1])
             else:
                 nc.gpsimd.tensor_scalar(
-                    out=w_rows[:],
+                    out=piece,
                     in0=piece,
                     scalar1=inverses[jt][:, 0:1],
                     scalar2=0.0,
                     op0=ALU.mult,
                     op1=ALU.add,
                 )
-            rows[u] = w_rows
 
         def flip(u):
-            w_flip = psum_ring.tile([P, PAIR, PACK, P], BF16, tag="ring")
+            jt, h = divmod(u, TILE_UNITS)
+            banks = []
             for a in range(PAIR):
+                w_flip = psum_ring.tile([P, PACK, P], F32, tag="ring")
                 for t in range(PACK):
-                    first = (PACK * a + t) * P
-                    nc.tensor.transpose(w_flip[:, a, t, :], rows[u][:, first : first + P], ident_bf16[:])
-            flips[u] = w_flip
+                    first = h * UNIT_COLS + (PACK * a + t) * P
+                    nc.tensor.transpose(w_flip[:, t, :], k_tiles[jt][:, first : first + P], ident_f32[:])
+                banks.append(w_flip)
+            flips[u] = banks
 
         def empty(u):
             w_grouped = work.tile([P, PAIR, P, PACK], BF16, align_bytes=64, bufs=4)
-            source = flips[u][:].rearrange("p a t j -> p a j t")
-            if scalar_helps(u):
-                nc.scalar.copy(out=w_grouped[:], in_=source)
-            else:
-                nc.vector.tensor_copy(out=w_grouped[:], in_=source)
+            for a in range(PAIR):
+                source = flips[u][a][:].rearrange("p t j -> p j t")
+                if scalar_helps(u):
+                    nc.scalar.copy(out=w_grouped[:, a, :, :], in_=source)
+                else:
+                    nc.vector.tensor_copy(out=w_grouped[:, a, :, :], in_=source)
             packs[u] = w_grouped
 
         def quantise(u):
@@ -291,7 +292,8 @@ def tile_rbfnet_pb_t_kernel(
             if s < UNITS:
                 if s % TILE_UNITS == 0:
                     invert_sum(s // TILE_UNITS)
-                normalise(s)
+                    for u in range(s, s + TILE_UNITS):
+                        normalise(u)
                 flip(s)
             if 0 <= s - LEAD < UNITS:
                 empty(s - LEAD)

@@ -43,7 +43,7 @@ def tile_rbfnet_pb_t_kernel(
         keep = ctx.enter_context(tc.tile_pool(name="keep", bufs=1))
         work = ctx.enter_context(tc.tile_pool(name="work", bufs=2))
         psum_ring = ctx.enter_context(tc.psum_pool(name="psum_ring", bufs=6))
-        psum_out = ctx.enter_context(tc.psum_pool(name="psum_out", bufs=2))
+        psum_one = ctx.enter_context(tc.psum_pool(name="psum_one", bufs=1))
         ctx.enter_context(tc.manual_schedule())
 
         x_sb = keep.tile([P, J_TILES, D], BF16)
@@ -196,6 +196,9 @@ def tile_rbfnet_pb_t_kernel(
                 )
 
         inverses = {}
+        inverse_wides = {}
+        inverse_flips = {}
+        inverse_rows = {}
         flips = {}
         packs = {}
         codes = {}
@@ -209,22 +212,25 @@ def tile_rbfnet_pb_t_kernel(
             nc.vector.reduce_sum(out=total[:], in_=k_sums[:, jt, :], axis=mybir.AxisListType.X)
             inverse = work.tile([P, 1], F32)
             nc.vector.reciprocal(out=inverse[:], in_=total[:])
+            inverse_wide = work.tile([P, P], F32)
+            nc.vector.tensor_copy(out=inverse_wide[:], in_=inverse[:, 0:1].to_broadcast([P, P]))
             inverses[jt] = inverse
+            inverse_wides[jt] = inverse_wide
+
+        def flip_inverse(jt):
+            inverse_flip = psum_one.tile([P, P], F32)
+            nc.tensor.transpose(inverse_flip[:], inverse_wides[jt][:], ident_f32[:])
+            inverse_flips[jt] = inverse_flip
+
+        def keep_inverse_row(jt):
+            inverse_row = work.tile([P, P], F32)
+            nc.vector.tensor_copy(out=inverse_row[:], in_=inverse_flips[jt][:])
+            inverse_rows[jt] = inverse_row
 
         def normalise(u):
             jt, h = divmod(u, TILE_UNITS)
             piece = k_tiles[jt][:, h * UNIT_COLS : (h + 1) * UNIT_COLS]
-            if scalar_helps(u):
-                nc.scalar.activation(out=piece, in_=piece, func=ACT.Copy, scale=inverses[jt][:, 0:1])
-            else:
-                nc.gpsimd.tensor_scalar(
-                    out=piece,
-                    in0=piece,
-                    scalar1=inverses[jt][:, 0:1],
-                    scalar2=0.0,
-                    op0=ALU.mult,
-                    op1=ALU.add,
-                )
+            nc.scalar.activation(out=piece, in_=piece, func=ACT.Copy, scale=inverses[jt][:, 0:1])
 
         def flip(u):
             jt, h = divmod(u, TILE_UNITS)
@@ -238,13 +244,19 @@ def tile_rbfnet_pb_t_kernel(
             flips[u] = banks
 
         def empty(u):
+            jt = u // TILE_UNITS
             w_grouped = work.tile([P, PAIR, P, PACK], BF16, align_bytes=64, bufs=4)
             for a in range(PAIR):
                 source = flips[u][a][:].rearrange("p t j -> p j t")
                 if scalar_helps(u):
                     nc.scalar.copy(out=w_grouped[:, a, :, :], in_=source)
                 else:
-                    nc.vector.tensor_copy(out=w_grouped[:, a, :, :], in_=source)
+                    nc.vector.tensor_tensor(
+                        out=w_grouped[:, a, :, :],
+                        in0=source,
+                        in1=inverse_rows[jt][:].unsqueeze(2).to_broadcast([P, P, PACK]),
+                        op=ALU.mult,
+                    )
             packs[u] = w_grouped
 
         def quantise(u):
@@ -261,7 +273,7 @@ def tile_rbfnet_pb_t_kernel(
             jt, h = divmod(u, TILE_UNITS)
             w_codes, w_planes = codes[u]
             if h == 0:
-                out_acc = psum_out.tile([P, C], F32)
+                out_acc = psum_one.tile([P, C], F32)
                 sums[jt] = out_acc
             for a in range(PAIR):
                 g = PAIR * h + a
@@ -289,12 +301,16 @@ def tile_rbfnet_pb_t_kernel(
         kernel_values(2)
         kernel_values(3)
         for s in range(UNITS + LEAD + 2):
-            if s < UNITS:
-                if s % TILE_UNITS == 0:
-                    invert_sum(s // TILE_UNITS)
-                    for u in range(s, s + TILE_UNITS):
+            new_tile = s < UNITS and s % TILE_UNITS == 1
+            if new_tile:
+                invert_sum(s // TILE_UNITS)
+                for u in range(s, s + TILE_UNITS - 1):
+                    if scalar_helps(u):
                         normalise(u)
+            if s < UNITS:
                 flip(s)
+            if new_tile:
+                flip_inverse(s // TILE_UNITS)
             if 0 <= s - LEAD < UNITS:
                 empty(s - LEAD)
             ready = s - LEAD - 1
@@ -305,3 +321,5 @@ def tile_rbfnet_pb_t_kernel(
                         multiply(u)
             if ready - 1 >= 0 and (ready - 1) % TILE_UNITS == TILE_UNITS - 1:
                 store((ready - 1) // TILE_UNITS)
+            if new_tile:
+                keep_inverse_row(s // TILE_UNITS)

@@ -31,6 +31,7 @@ EXP_COLS = 2048
 WORD_LOAD_COLS = 1024
 PLANE_COLS = NTR // 4
 SQRT_FLOOR = 2.0 ** -100
+SQRT_CEILING = 2.0 ** 118
 
 FLOPS = 2 * NTR * NTE * D + 2 * NTE * NTR * C
 
@@ -107,10 +108,20 @@ def tile_rbfnet_pb_t_kernel(
         for t in range(PACK):
             nc.tensor.transpose(vec_flip[:, t, :], vec_rows[:, t:K_PASS:PACK], ident_bf16[:])
         nc.tensor.transpose(vec_flip[:, PACK, :], vec_rows[:, 0:P], ident_bf16[:])
-        nc.vector.tensor_copy(
-            out=s_cols[:], in_=vec_flip[:, 0:PACK, 0:GROUPS].rearrange("p t g -> p g t")
+        nc.vector.tensor_scalar(
+            out=s_cols[:],
+            in0=vec_flip[:, 0:PACK, 0:GROUPS].rearrange("p t g -> p g t"),
+            scalar1=0.5,
+            scalar2=None,
+            op0=ALU.mult,
         )
-        nc.vector.tensor_copy(out=c_cols[:], in_=vec_flip[:, PACK, GROUPS : GROUPS + J_TILES])
+        nc.vector.tensor_scalar(
+            out=c_cols[:],
+            in0=vec_flip[:, PACK, GROUPS : GROUPS + J_TILES],
+            scalar1=0.5,
+            scalar2=None,
+            op0=ALU.mult,
+        )
         x_grouped_words = x_grouped[:].bitcast(F32).rearrange("p (a j u) -> p a j u", a=J_TILES, u=2)
         for pair in range(J_TILES // 2):
             x_flip = psum_ring.tile([P, 2, 2, P], F32, tag="ring")
@@ -144,15 +155,15 @@ def tile_rbfnet_pb_t_kernel(
         def clamp_and_root(batch, done):
             for jt in batch:
                 piece = k_tiles[jt][:, done - CLAMP_COLS : done]
-                nc.vector.tensor_scalar(
+                nc.gpsimd.tensor_scalar(
                     out=piece,
                     in0=piece,
-                    scalar1=c_cols[:, jt : jt + 1],
-                    scalar2=SQRT_FLOOR,
-                    op0=ALU.add,
+                    scalar1=-0.5 * SQRT_FLOOR,
+                    scalar2=-0.5 * SQRT_CEILING,
+                    op0=ALU.min,
                     op1=ALU.max,
                 )
-                nc.scalar.activation(out=piece, in_=piece, func=ACT.Sqrt)
+                nc.scalar.activation(out=piece, in_=piece, func=ACT.Sqrt, scale=-2.0)
 
         def distances(batch):
             for g in range(GROUPS):
@@ -175,14 +186,13 @@ def tile_rbfnet_pb_t_kernel(
                     nc.vector.scalar_tensor_tensor(
                         out=k_tiles[jt][:, cols].rearrange("p (t n) -> p t n", t=PACK),
                         in0=cross[:].rearrange("p (n t) -> p t n", t=PACK),
-                        scalar=-2.0,
+                        scalar=c_cols[:, jt : jt + 1],
                         in1=s_all[:, g, :, :],
-                        op0=ALU.mult,
-                        op1=ALU.add,
+                        op0=ALU.subtract,
+                        op1=ALU.subtract,
                     )
-                if g > 0 and (g * K_PASS) % CLAMP_COLS == 0:
-                    clamp_and_root(batch, g * K_PASS)
-            clamp_and_root(batch, NTR)
+                if ((g + 1) * K_PASS) % CLAMP_COLS == 0:
+                    clamp_and_root(batch, (g + 1) * K_PASS)
 
         def kernel_values(jt):
             for e in range(NTR // EXP_COLS):

@@ -21,14 +21,16 @@ J_TILES = NTE // P
 GROUPS = NTR // K_PASS
 PAIR = 2
 UNIT_COLS = PAIR * K_PASS
+UNIT_BLOCKS = UNIT_COLS // (2 * P)
 TILE_UNITS = NTR // UNIT_COLS
 UNITS = J_TILES * TILE_UNITS
-LEAD = 2
 BURST = 4
-HELP_FROM = 21
 CLAMP_COLS = 1024
 EXP_COLS = 2048
+EXP_PIECES = NTR // EXP_COLS
 WORD_LOAD_COLS = 1024
+S_LOAD_COLS = 2048
+GROUPS_PER_S_LOAD = S_LOAD_COLS // K_PASS
 PLANE_COLS = NTR // 4
 SQRT_FLOOR = 2.0 ** -100
 SQRT_CEILING = 2.0 ** 118
@@ -44,7 +46,7 @@ def tile_rbfnet_pb_t_kernel(
         keep = ctx.enter_context(tc.tile_pool(name="keep", bufs=1))
         work = ctx.enter_context(tc.tile_pool(name="work", bufs=2))
         psum_ring = ctx.enter_context(tc.psum_pool(name="psum_ring", bufs=6))
-        psum_one = ctx.enter_context(tc.psum_pool(name="psum_one", bufs=1))
+        psum_sums = ctx.enter_context(tc.psum_pool(name="psum_sums", bufs=2))
         ctx.enter_context(tc.manual_schedule())
 
         x_sb = keep.tile([P, J_TILES, D], BF16)
@@ -55,17 +57,16 @@ def tile_rbfnet_pb_t_kernel(
         sm_planes = keep.tile([P, PLANE_COLS], U8, align_bytes=64)
         y_codes = keep.tile([P, GROUPS, C], U32, align_bytes=64)
         y_planes = keep.tile([P, GROUPS, C], U8, align_bytes=64)
-        vec_rows = keep.tile([P, K_PASS], BF16)
-        s_cols = keep.tile([P, GROUPS, PACK], BF16)
+        c_rows = keep.tile([P, P], BF16)
         c_cols = keep.tile([P, J_TILES], F32)
-        s_all = keep.tile([P, GROUPS, PACK, P], BF16)
+        s_half = keep.tile([P, NTR], BF16)
         ident_f32 = keep.tile([P, P], F32)
         ident_bf16 = keep.tile([P, P], BF16)
         warm = keep.tile([P, 2], F32)
         k_sums = keep.tile([P, J_TILES, NTR // EXP_COLS], F32)
         k_tiles = [keep.tile([P, NTR], F32, name="k_tile%d" % jt) for jt in range(J_TILES)]
 
-        nc.vector.memset(vec_rows[:], 0.0)
+        nc.vector.memset(c_rows[:], 0.0)
         nc.vector.memset(sm_planes[:].bitcast(I32), 0)
         nc.vector.memset(warm[:], 1.0)
         nc.vector.memset(y_planes[:].rearrange("p g c -> p (g c)").bitcast(I32), 0)
@@ -73,12 +74,19 @@ def tile_rbfnet_pb_t_kernel(
         make_identity(nc, ident_f32[:])
         nc.scalar.activation(out=warm[:, 1:2], in_=warm[:, 0:1], func=ACT.Sqrt)
 
-        nc.sync.dma_start(out=vec_rows[0:GROUPS, :], in_=s_norm2.rearrange("(g n) -> g n", g=GROUPS))
-        nc.sync.dma_start(
-            out=vec_rows[GROUPS : GROUPS + J_TILES, 0:P],
-            in_=c_norm2.rearrange("(a n) -> a n", a=J_TILES),
-        )
+        def load_s(k):
+            cols = slice(k * S_LOAD_COLS, (k + 1) * S_LOAD_COLS)
+            nc.sync.dma_start(out=s_half[:, cols], in_=s_norm2[cols].partition_broadcast(P))
+
+        def halve_s(k):
+            cols = slice(k * S_LOAD_COLS, (k + 1) * S_LOAD_COLS)
+            nc.vector.tensor_scalar(
+                out=s_half[:, cols], in0=s_half[:, cols], scalar1=0.5, scalar2=None, op0=ALU.mult
+            )
+
+        nc.sync.dma_start(out=c_rows[0:J_TILES, :], in_=c_norm2.rearrange("(a n) -> a n", a=J_TILES))
         nc.sync.dma_start(out=x_sb[:], in_=x_test.rearrange("(a p) k -> p a k", p=P))
+        load_s(0)
         for quadrant in range(4):
             nc.sync.dma_start(
                 out=sm_planes[32 * quadrant : 32 * quadrant + 16, :].bitcast(I32),
@@ -92,6 +100,8 @@ def tile_rbfnet_pb_t_kernel(
                 out=sm_codes[:, first : first + WORD_LOAD_COLS].bitcast(I32),
                 in_=sm_word_bytes[:, PACK * first : PACK * (first + WORD_LOAD_COLS)].bitcast(I32),
             )
+            if first % S_LOAD_COLS == 0 and first // S_LOAD_COLS + 1 < NTR // S_LOAD_COLS:
+                load_s(first // S_LOAD_COLS + 1)
         for quadrant in range(4):
             nc.sync.dma_start(
                 out=y_planes[32 * quadrant : 32 * quadrant + 4, :, :].bitcast(I32),
@@ -104,23 +114,10 @@ def tile_rbfnet_pb_t_kernel(
             in_=y_train_words.rearrange("g p n t -> p g (n t)").bitcast(I32),
         )
 
-        vec_flip = psum_ring.tile([P, PACK + 1, P], BF16, tag="ring")
-        for t in range(PACK):
-            nc.tensor.transpose(vec_flip[:, t, :], vec_rows[:, t:K_PASS:PACK], ident_bf16[:])
-        nc.tensor.transpose(vec_flip[:, PACK, :], vec_rows[:, 0:P], ident_bf16[:])
+        c_flip = psum_ring.tile([P, P], BF16, tag="ring")
+        nc.tensor.transpose(c_flip[:], c_rows[:], ident_bf16[:])
         nc.vector.tensor_scalar(
-            out=s_cols[:],
-            in0=vec_flip[:, 0:PACK, 0:GROUPS].rearrange("p t g -> p g t"),
-            scalar1=0.5,
-            scalar2=None,
-            op0=ALU.mult,
-        )
-        nc.vector.tensor_scalar(
-            out=c_cols[:],
-            in0=vec_flip[:, PACK, GROUPS : GROUPS + J_TILES],
-            scalar1=0.5,
-            scalar2=None,
-            op0=ALU.mult,
+            out=c_cols[:], in0=c_flip[:, 0:J_TILES], scalar1=0.5, scalar2=None, op0=ALU.mult
         )
         x_grouped_words = x_grouped[:].bitcast(F32).rearrange("p (a j u) -> p a j u", a=J_TILES, u=2)
         for pair in range(J_TILES // 2):
@@ -139,19 +136,6 @@ def tile_rbfnet_pb_t_kernel(
 
         nc.vector.quantize_mx(out=x_codes[:].bitcast(FP8X4), scales=x_planes[:], in_=x_grouped[:])
 
-        def spread_s(pair):
-            s_bank = psum_ring.tile([P, 2, PACK, P], BF16, tag="ring")
-            for a in range(2):
-                for t in range(PACK):
-                    nc.tensor.matmul(
-                        out=s_bank[:, a, t, :],
-                        lhsT=s_cols[:, 2 * pair + a, t : t + 1].to_broadcast([P, P]),
-                        rhs=ident_bf16[:],
-                        start=True,
-                        stop=True,
-                    )
-            nc.scalar.copy(out=s_all[:, 2 * pair : 2 * pair + 2, :, :], in_=s_bank[:])
-
         def clamp_and_root(batch, done):
             for jt in batch:
                 piece = k_tiles[jt][:, done - CLAMP_COLS : done]
@@ -167,8 +151,8 @@ def tile_rbfnet_pb_t_kernel(
 
         def distances(batch):
             for g in range(GROUPS):
-                if batch[0] == 0 and g + 2 < GROUPS // 2:
-                    spread_s(g + 2)
+                if batch[0] == 0 and g % GROUPS_PER_S_LOAD == GROUPS_PER_S_LOAD - 2 and g + 2 < GROUPS:
+                    halve_s((g + 2) // GROUPS_PER_S_LOAD)
                 cols = slice(g * K_PASS, (g + 1) * K_PASS)
                 quarter, first = divmod(g * K_PASS, PLANE_COLS)
                 plane_cols = slice(first, first + K_PASS)
@@ -187,86 +171,78 @@ def tile_rbfnet_pb_t_kernel(
                         out=k_tiles[jt][:, cols].rearrange("p (t n) -> p t n", t=PACK),
                         in0=cross[:].rearrange("p (n t) -> p t n", t=PACK),
                         scalar=c_cols[:, jt : jt + 1],
-                        in1=s_all[:, g, :, :],
+                        in1=s_half[:, cols].rearrange("p (n t) -> p t n", t=PACK),
                         op0=ALU.subtract,
                         op1=ALU.subtract,
                     )
                 if ((g + 1) * K_PASS) % CLAMP_COLS == 0:
                     clamp_and_root(batch, (g + 1) * K_PASS)
 
+        def kernel_piece(jt, e):
+            piece = k_tiles[jt][:, e * EXP_COLS : (e + 1) * EXP_COLS]
+            nc.scalar.activation(
+                out=piece,
+                in_=piece,
+                func=ACT.Exp,
+                scale=-1.0 / GAMMA,
+                accum_out=k_sums[:, jt, e : e + 1],
+            )
+
         def kernel_values(jt):
-            for e in range(NTR // EXP_COLS):
-                piece = k_tiles[jt][:, e * EXP_COLS : (e + 1) * EXP_COLS]
-                nc.scalar.activation(
-                    out=piece,
-                    in_=piece,
-                    func=ACT.Exp,
-                    scale=-1.0 / GAMMA,
-                    accum_out=k_sums[:, jt, e : e + 1],
-                )
+            for e in range(EXP_PIECES):
+                kernel_piece(jt, e)
 
         inverses = {}
-        inverse_wides = {}
-        inverse_flips = {}
-        inverse_rows = {}
+        pairs = {}
         flips = {}
         packs = {}
         codes = {}
         sums = {}
 
-        def scalar_helps(u):
-            return u >= HELP_FROM and u % 2 == 1
+        def scalar_empties(u):
+            return u >= 3 * TILE_UNITS or (u >= 2 * TILE_UNITS and u % 2 == 0)
 
         def invert_sum(jt):
             total = work.tile([P, 1], F32)
             nc.vector.reduce_sum(out=total[:], in_=k_sums[:, jt, :], axis=mybir.AxisListType.X)
             inverse = work.tile([P, 1], F32)
             nc.vector.reciprocal(out=inverse[:], in_=total[:])
-            inverse_wide = work.tile([P, P], F32)
-            nc.vector.tensor_copy(out=inverse_wide[:], in_=inverse[:, 0:1].to_broadcast([P, P]))
             inverses[jt] = inverse
-            inverse_wides[jt] = inverse_wide
-
-        def flip_inverse(jt):
-            inverse_flip = psum_one.tile([P, P], F32)
-            nc.tensor.transpose(inverse_flip[:], inverse_wides[jt][:], ident_f32[:])
-            inverse_flips[jt] = inverse_flip
-
-        def keep_inverse_row(jt):
-            inverse_row = work.tile([P, P], F32)
-            nc.vector.tensor_copy(out=inverse_row[:], in_=inverse_flips[jt][:])
-            inverse_rows[jt] = inverse_row
 
         def normalise(u):
             jt, h = divmod(u, TILE_UNITS)
-            piece = k_tiles[jt][:, h * UNIT_COLS : (h + 1) * UNIT_COLS]
-            nc.scalar.activation(out=piece, in_=piece, func=ACT.Copy, scale=inverses[jt][:, 0:1])
+            w_pairs = work.tile([P, UNIT_COLS], BF16, bufs=3)
+            nc.vector.tensor_scalar(
+                out=w_pairs[:].rearrange("p (b n e) -> p b n e", b=UNIT_BLOCKS, e=2),
+                in0=k_tiles[jt][:, h * UNIT_COLS : (h + 1) * UNIT_COLS].rearrange(
+                    "p (b e n) -> p b n e", b=UNIT_BLOCKS, e=2
+                ),
+                scalar1=inverses[jt][:, 0:1],
+                scalar2=None,
+                op0=ALU.mult,
+            )
+            pairs[u] = w_pairs
 
         def flip(u):
-            jt, h = divmod(u, TILE_UNITS)
-            banks = []
-            for a in range(PAIR):
-                w_flip = psum_ring.tile([P, PACK, P], F32, tag="ring")
-                for t in range(PACK):
-                    first = h * UNIT_COLS + (PACK * a + t) * P
-                    nc.tensor.transpose(w_flip[:, t, :], k_tiles[jt][:, first : first + P], ident_f32[:])
-                banks.append(w_flip)
-            flips[u] = banks
+            w_flip = psum_ring.tile([P, UNIT_BLOCKS, P], F32, tag="ring")
+            words = pairs[u][:].bitcast(F32)
+            for b in range(UNIT_BLOCKS):
+                nc.tensor.transpose(w_flip[:, b, :], words[:, b * P : (b + 1) * P], ident_f32[:])
+            flips[u] = w_flip
 
         def empty(u):
-            jt = u // TILE_UNITS
             w_grouped = work.tile([P, PAIR, P, PACK], BF16, align_bytes=64, bufs=4)
-            for a in range(PAIR):
-                source = flips[u][a][:].rearrange("p t j -> p j t")
-                if scalar_helps(u):
-                    nc.scalar.copy(out=w_grouped[:, a, :, :], in_=source)
-                else:
-                    nc.vector.tensor_tensor(
-                        out=w_grouped[:, a, :, :],
-                        in0=source,
-                        in1=inverse_rows[jt][:].unsqueeze(2).to_broadcast([P, P, PACK]),
-                        op=ALU.mult,
-                    )
+            target = (
+                w_grouped[:]
+                .rearrange("p a j t -> p (a j t)")
+                .bitcast(F32)
+                .rearrange("p (a j u) -> p a j u", a=PAIR, u=2)
+            )
+            source = flips[u][:].rearrange("p (a u) j -> p a j u", u=2)
+            if scalar_empties(u):
+                nc.scalar.copy(out=target, in_=source)
+            else:
+                nc.vector.tensor_copy(out=target, in_=source)
             packs[u] = w_grouped
 
         def quantise(u):
@@ -283,7 +259,7 @@ def tile_rbfnet_pb_t_kernel(
             jt, h = divmod(u, TILE_UNITS)
             w_codes, w_planes = codes[u]
             if h == 0:
-                out_acc = psum_one.tile([P, C], F32)
+                out_acc = psum_sums.tile([P, C], F32)
                 sums[jt] = out_acc
             for a in range(PAIR):
                 g = PAIR * h + a
@@ -302,28 +278,24 @@ def tile_rbfnet_pb_t_kernel(
             nc.vector.tensor_copy(out=out_sb[:], in_=sums[jt][:])
             nc.sync.dma_start(out=out[jt * P : (jt + 1) * P, :], in_=out_sb[:])
 
-        spread_s(0)
-        spread_s(1)
+        halve_s(0)
         distances((0, 1))
         kernel_values(0)
         kernel_values(1)
         distances((2, 3))
         kernel_values(2)
-        kernel_values(3)
-        for s in range(UNITS + LEAD + 2):
-            new_tile = s < UNITS and s % TILE_UNITS == 1
-            if new_tile:
-                invert_sum(s // TILE_UNITS)
-                for u in range(s, s + TILE_UNITS - 1):
-                    if scalar_helps(u):
-                        normalise(u)
+        for s in range(UNITS + 3):
             if s < UNITS:
+                jt, h = divmod(s, TILE_UNITS)
+                if jt == J_TILES - 2 and h % 2 == 0:
+                    kernel_piece(J_TILES - 1, h // 2)
+                if h == 0:
+                    invert_sum(jt)
+                normalise(s)
                 flip(s)
-            if new_tile:
-                flip_inverse(s // TILE_UNITS)
-            if 0 <= s - LEAD < UNITS:
-                empty(s - LEAD)
-            ready = s - LEAD - 1
+            if 0 <= s - 1 < UNITS:
+                empty(s - 1)
+            ready = s - 2
             if 0 <= ready < UNITS:
                 quantise(ready)
                 if ready % BURST == BURST - 1:
@@ -331,5 +303,3 @@ def tile_rbfnet_pb_t_kernel(
                         multiply(u)
             if ready - 1 >= 0 and (ready - 1) % TILE_UNITS == TILE_UNITS - 1:
                 store((ready - 1) // TILE_UNITS)
-            if new_tile:
-                keep_inverse_row(s // TILE_UNITS)

@@ -29,8 +29,6 @@ CLAMP_COLS = 1024
 EXP_COLS = 2048
 EXP_PIECES = NTR // EXP_COLS
 WORD_LOAD_COLS = 1024
-S_LOAD_COLS = 2048
-GROUPS_PER_S_LOAD = S_LOAD_COLS // K_PASS
 PLANE_COLS = NTR // 4
 SQRT_FLOOR = 2.0 ** -100
 SQRT_CEILING = 2.0 ** 118
@@ -57,16 +55,17 @@ def tile_rbfnet_pb_t_kernel(
         sm_planes = keep.tile([P, PLANE_COLS], U8, align_bytes=64)
         y_codes = keep.tile([P, GROUPS, C], U32, align_bytes=64)
         y_planes = keep.tile([P, GROUPS, C], U8, align_bytes=64)
-        c_rows = keep.tile([P, P], BF16)
+        vec_rows = keep.tile([P, K_PASS], BF16)
+        s_cols = keep.tile([P, GROUPS, PACK], BF16)
         c_cols = keep.tile([P, J_TILES], F32)
-        s_half = keep.tile([P, NTR], BF16)
+        s_all = keep.tile([P, GROUPS, PACK, P], BF16)
         ident_f32 = keep.tile([P, P], F32)
         ident_bf16 = keep.tile([P, P], BF16)
         warm = keep.tile([P, 2], F32)
         k_sums = keep.tile([P, J_TILES, NTR // EXP_COLS], F32)
         k_tiles = [keep.tile([P, NTR], F32, name="k_tile%d" % jt) for jt in range(J_TILES)]
 
-        nc.vector.memset(c_rows[:], 0.0)
+        nc.vector.memset(vec_rows[:], 0.0)
         nc.vector.memset(sm_planes[:].bitcast(I32), 0)
         nc.vector.memset(warm[:], 1.0)
         nc.vector.memset(y_planes[:].rearrange("p g c -> p (g c)").bitcast(I32), 0)
@@ -74,19 +73,12 @@ def tile_rbfnet_pb_t_kernel(
         make_identity(nc, ident_f32[:])
         nc.scalar.activation(out=warm[:, 1:2], in_=warm[:, 0:1], func=ACT.Sqrt)
 
-        def load_s(k):
-            cols = slice(k * S_LOAD_COLS, (k + 1) * S_LOAD_COLS)
-            nc.sync.dma_start(out=s_half[:, cols], in_=s_norm2[cols].partition_broadcast(P))
-
-        def halve_s(k):
-            cols = slice(k * S_LOAD_COLS, (k + 1) * S_LOAD_COLS)
-            nc.vector.tensor_scalar(
-                out=s_half[:, cols], in0=s_half[:, cols], scalar1=0.5, scalar2=None, op0=ALU.mult
-            )
-
-        nc.sync.dma_start(out=c_rows[0:J_TILES, :], in_=c_norm2.rearrange("(a n) -> a n", a=J_TILES))
+        nc.sync.dma_start(out=vec_rows[0:GROUPS, :], in_=s_norm2.rearrange("(g n) -> g n", g=GROUPS))
+        nc.sync.dma_start(
+            out=vec_rows[GROUPS : GROUPS + J_TILES, 0:P],
+            in_=c_norm2.rearrange("(a n) -> a n", a=J_TILES),
+        )
         nc.sync.dma_start(out=x_sb[:], in_=x_test.rearrange("(a p) k -> p a k", p=P))
-        load_s(0)
         for quadrant in range(4):
             nc.sync.dma_start(
                 out=sm_planes[32 * quadrant : 32 * quadrant + 16, :].bitcast(I32),
@@ -100,8 +92,6 @@ def tile_rbfnet_pb_t_kernel(
                 out=sm_codes[:, first : first + WORD_LOAD_COLS].bitcast(I32),
                 in_=sm_word_bytes[:, PACK * first : PACK * (first + WORD_LOAD_COLS)].bitcast(I32),
             )
-            if first % S_LOAD_COLS == 0 and first // S_LOAD_COLS + 1 < NTR // S_LOAD_COLS:
-                load_s(first // S_LOAD_COLS + 1)
         for quadrant in range(4):
             nc.sync.dma_start(
                 out=y_planes[32 * quadrant : 32 * quadrant + 4, :, :].bitcast(I32),
@@ -114,10 +104,23 @@ def tile_rbfnet_pb_t_kernel(
             in_=y_train_words.rearrange("g p n t -> p g (n t)").bitcast(I32),
         )
 
-        c_flip = psum_ring.tile([P, P], BF16, tag="ring")
-        nc.tensor.transpose(c_flip[:], c_rows[:], ident_bf16[:])
+        vec_flip = psum_ring.tile([P, PACK + 1, P], BF16, tag="ring")
+        for t in range(PACK):
+            nc.tensor.transpose(vec_flip[:, t, :], vec_rows[:, t:K_PASS:PACK], ident_bf16[:])
+        nc.tensor.transpose(vec_flip[:, PACK, :], vec_rows[:, 0:P], ident_bf16[:])
         nc.vector.tensor_scalar(
-            out=c_cols[:], in0=c_flip[:, 0:J_TILES], scalar1=0.5, scalar2=None, op0=ALU.mult
+            out=s_cols[:],
+            in0=vec_flip[:, 0:PACK, 0:GROUPS].rearrange("p t g -> p g t"),
+            scalar1=0.5,
+            scalar2=None,
+            op0=ALU.mult,
+        )
+        nc.vector.tensor_scalar(
+            out=c_cols[:],
+            in0=vec_flip[:, PACK, GROUPS : GROUPS + J_TILES],
+            scalar1=0.5,
+            scalar2=None,
+            op0=ALU.mult,
         )
         x_grouped_words = x_grouped[:].bitcast(F32).rearrange("p (a j u) -> p a j u", a=J_TILES, u=2)
         for pair in range(J_TILES // 2):
@@ -136,6 +139,19 @@ def tile_rbfnet_pb_t_kernel(
 
         nc.vector.quantize_mx(out=x_codes[:].bitcast(FP8X4), scales=x_planes[:], in_=x_grouped[:])
 
+        def spread_s(pair):
+            s_bank = psum_ring.tile([P, 2, PACK, P], BF16, tag="ring")
+            for a in range(2):
+                for t in range(PACK):
+                    nc.tensor.matmul(
+                        out=s_bank[:, a, t, :],
+                        lhsT=s_cols[:, 2 * pair + a, t : t + 1].to_broadcast([P, P]),
+                        rhs=ident_bf16[:],
+                        start=True,
+                        stop=True,
+                    )
+            nc.scalar.copy(out=s_all[:, 2 * pair : 2 * pair + 2, :, :], in_=s_bank[:])
+
         def clamp_and_root(batch, done):
             for jt in batch:
                 piece = k_tiles[jt][:, done - CLAMP_COLS : done]
@@ -151,8 +167,8 @@ def tile_rbfnet_pb_t_kernel(
 
         def distances(batch):
             for g in range(GROUPS):
-                if batch[0] == 0 and g % GROUPS_PER_S_LOAD == GROUPS_PER_S_LOAD - 2 and g + 2 < GROUPS:
-                    halve_s((g + 2) // GROUPS_PER_S_LOAD)
+                if batch[0] == 0 and g + 2 < GROUPS // 2:
+                    spread_s(g + 2)
                 cols = slice(g * K_PASS, (g + 1) * K_PASS)
                 quarter, first = divmod(g * K_PASS, PLANE_COLS)
                 plane_cols = slice(first, first + K_PASS)
@@ -171,7 +187,7 @@ def tile_rbfnet_pb_t_kernel(
                         out=k_tiles[jt][:, cols].rearrange("p (t n) -> p t n", t=PACK),
                         in0=cross[:].rearrange("p (n t) -> p t n", t=PACK),
                         scalar=c_cols[:, jt : jt + 1],
-                        in1=s_half[:, cols].rearrange("p (n t) -> p t n", t=PACK),
+                        in1=s_all[:, g, :, :],
                         op0=ALU.subtract,
                         op1=ALU.subtract,
                     )
@@ -278,7 +294,8 @@ def tile_rbfnet_pb_t_kernel(
             nc.vector.tensor_copy(out=out_sb[:], in_=sums[jt][:])
             nc.sync.dma_start(out=out[jt * P : (jt + 1) * P, :], in_=out_sb[:])
 
-        halve_s(0)
+        spread_s(0)
+        spread_s(1)
         distances((0, 1))
         kernel_values(0)
         kernel_values(1)

@@ -24,6 +24,7 @@ UNIT_COLS = PAIR * K_PASS
 UNIT_BLOCKS = UNIT_COLS // (2 * P)
 TILE_UNITS = NTR // UNIT_COLS
 UNITS = J_TILES * TILE_UNITS
+LEAD = 2
 BURST = 4
 CLAMP_COLS = 1024
 EXP_COLS = 2048
@@ -227,7 +228,7 @@ def tile_rbfnet_pb_t_kernel(
 
         def normalise(u):
             jt, h = divmod(u, TILE_UNITS)
-            w_pairs = work.tile([P, UNIT_COLS], BF16, bufs=3)
+            w_pairs = work.tile([P, UNIT_COLS], BF16, bufs=LEAD + 2)
             nc.vector.tensor_scalar(
                 out=w_pairs[:].rearrange("p (b n e) -> p b n e", b=UNIT_BLOCKS, e=2),
                 in0=k_tiles[jt][:, h * UNIT_COLS : (h + 1) * UNIT_COLS].rearrange(
@@ -301,22 +302,23 @@ def tile_rbfnet_pb_t_kernel(
         kernel_values(1)
         distances((2, 3))
         kernel_values(2)
-        for s in range(UNITS + 3):
-            if s < UNITS:
-                jt, h = divmod(s, TILE_UNITS)
-                if jt == J_TILES - 2 and h % 2 == 0:
-                    kernel_piece(J_TILES - 1, h // 2)
-                if h == 0:
-                    invert_sum(jt)
-                normalise(s)
-                flip(s)
-            if 0 <= s - 1 < UNITS:
-                empty(s - 1)
-            ready = s - 2
-            if 0 <= ready < UNITS:
-                quantise(ready)
-                if ready % BURST == BURST - 1:
-                    for u in range(ready - BURST + 1, ready + 1):
-                        multiply(u)
-            if ready - 1 >= 0 and (ready - 1) % TILE_UNITS == TILE_UNITS - 1:
-                store((ready - 1) // TILE_UNITS)
+        waiting = []
+        for jt in range(J_TILES):
+            first = jt * TILE_UNITS
+            invert_sum(jt)
+            for k in range(TILE_UNITS + LEAD + 1):
+                if jt == J_TILES - 2 and k % 2 == 1 and k // 2 < EXP_PIECES:
+                    kernel_piece(J_TILES - 1, k // 2)
+                if k < TILE_UNITS:
+                    normalise(first + k)
+                    flip(first + k)
+                if 0 <= k - LEAD < TILE_UNITS:
+                    empty(first + k - LEAD)
+                if k - LEAD - 1 >= 0:
+                    quantise(first + k - LEAD - 1)
+                    waiting.append(first + k - LEAD - 1)
+                    if len(waiting) == BURST or k >= TILE_UNITS - 1:
+                        for u in waiting:
+                            multiply(u)
+                        waiting.clear()
+            store(jt)

@@ -25,6 +25,8 @@ UNIT_BLOCKS = UNIT_COLS // (2 * P)
 TILE_UNITS = NTR // UNIT_COLS
 UNITS = J_TILES * TILE_UNITS
 LEAD = 2
+SHARED_UNITS = (0, 2, 3, 5)
+EXP_STEPS = (0, 3, 6, 8)
 BURST = 4
 CLAMP_COLS = 1024
 EXP_COLS = 2048
@@ -79,7 +81,14 @@ def tile_rbfnet_pb_t_kernel(
             out=vec_rows[GROUPS : GROUPS + J_TILES, 0:P],
             in_=c_norm2.rearrange("(a n) -> a n", a=J_TILES),
         )
-        nc.sync.dma_start(out=x_sb[:], in_=x_test.rearrange("(a p) k -> p a k", p=P))
+
+        def load_x(pair):
+            nc.sync.dma_start(
+                out=x_sb[:, 2 * pair : 2 * pair + 2, :],
+                in_=x_test[2 * pair * P : (2 * pair + 2) * P, :].rearrange("(a p) k -> p a k", p=P),
+            )
+
+        load_x(0)
         for quadrant in range(4):
             nc.sync.dma_start(
                 out=sm_planes[32 * quadrant : 32 * quadrant + 16, :].bitcast(I32),
@@ -93,6 +102,8 @@ def tile_rbfnet_pb_t_kernel(
                 out=sm_codes[:, first : first + WORD_LOAD_COLS].bitcast(I32),
                 in_=sm_word_bytes[:, PACK * first : PACK * (first + WORD_LOAD_COLS)].bitcast(I32),
             )
+            if first == 0:
+                load_x(1)
         for quadrant in range(4):
             nc.sync.dma_start(
                 out=y_planes[32 * quadrant : 32 * quadrant + 4, :, :].bitcast(I32),
@@ -123,22 +134,6 @@ def tile_rbfnet_pb_t_kernel(
             scalar2=None,
             op0=ALU.mult,
         )
-        x_grouped_words = x_grouped[:].bitcast(F32).rearrange("p (a j u) -> p a j u", a=J_TILES, u=2)
-        for pair in range(J_TILES // 2):
-            x_flip = psum_ring.tile([P, 2, 2, P], F32, tag="ring")
-            for a in range(2):
-                for u in range(2):
-                    nc.tensor.transpose(
-                        x_flip[:, a, u, :],
-                        x_sb[:, 2 * pair + a, :].bitcast(F32)[:, u : D // 2 : 2],
-                        ident_f32[:],
-                    )
-            nc.vector.tensor_copy(
-                out=x_grouped_words[:, 2 * pair : 2 * pair + 2, :, :],
-                in_=x_flip[:].rearrange("p a u j -> p a j u"),
-            )
-
-        nc.vector.quantize_mx(out=x_codes[:].bitcast(FP8X4), scales=x_planes[:], in_=x_grouped[:])
 
         def spread_s(pair):
             s_bank = psum_ring.tile([P, 2, PACK, P], BF16, tag="ring")
@@ -153,9 +148,32 @@ def tile_rbfnet_pb_t_kernel(
                     )
             nc.scalar.copy(out=s_all[:, 2 * pair : 2 * pair + 2, :, :], in_=s_bank[:])
 
-        def clamp_and_root(batch, done):
+        x_grouped_words = x_grouped[:].bitcast(F32).rearrange("p (a j u) -> p a j u", a=J_TILES, u=2)
+
+        def flip_x(pair, copy_out):
+            x_flip = psum_ring.tile([P, 2, 2, P], F32, tag="ring")
+            for a in range(2):
+                for u in range(2):
+                    nc.tensor.transpose(
+                        x_flip[:, a, u, :],
+                        x_sb[:, 2 * pair + a, :].bitcast(F32)[:, u : D // 2 : 2],
+                        ident_f32[:],
+                    )
+            copy_out(
+                out=x_grouped_words[:, 2 * pair : 2 * pair + 2, :, :],
+                in_=x_flip[:].rearrange("p a u j -> p a j u"),
+            )
+
+        def quantise_x(pair):
+            nc.vector.quantize_mx(
+                out=x_codes[:, 2 * pair * P : (2 * pair + 2) * P].bitcast(FP8X4),
+                scales=x_planes[:, 2 * pair * P : (2 * pair + 2) * P],
+                in_=x_grouped[:, 2 * pair * P * PACK : (2 * pair + 2) * P * PACK],
+            )
+
+        def clamp_and_root(batch, begun, done):
             for jt in batch:
-                piece = k_tiles[jt][:, done - CLAMP_COLS : done]
+                piece = k_tiles[jt][:, begun:done]
                 nc.gpsimd.tensor_scalar(
                     out=piece,
                     in0=piece,
@@ -167,9 +185,11 @@ def tile_rbfnet_pb_t_kernel(
                 nc.scalar.activation(out=piece, in_=piece, func=ACT.Sqrt, scale=-2.0)
 
         def distances(batch):
+            ends = list(range(CLAMP_COLS, NTR + 1, CLAMP_COLS))
+            if batch[0] == 0:
+                ends = [K_PASS] + ends + [NTR - K_PASS]
+            begun = 0
             for g in range(GROUPS):
-                if batch[0] == 0 and g + 2 < GROUPS // 2:
-                    spread_s(g + 2)
                 cols = slice(g * K_PASS, (g + 1) * K_PASS)
                 quarter, first = divmod(g * K_PASS, PLANE_COLS)
                 plane_cols = slice(first, first + K_PASS)
@@ -192,8 +212,16 @@ def tile_rbfnet_pb_t_kernel(
                         op0=ALU.subtract,
                         op1=ALU.subtract,
                     )
-                if ((g + 1) * K_PASS) % CLAMP_COLS == 0:
-                    clamp_and_root(batch, (g + 1) * K_PASS)
+                if batch[0] == 0:
+                    if g == 0:
+                        flip_x(1, nc.scalar.copy)
+                    if g + 2 < GROUPS // 2:
+                        spread_s(g + 2)
+                    if g == 3:
+                        quantise_x(1)
+                if (g + 1) * K_PASS in ends:
+                    clamp_and_root(batch, begun, (g + 1) * K_PASS)
+                    begun = (g + 1) * K_PASS
 
         def kernel_piece(jt, e):
             piece = k_tiles[jt][:, e * EXP_COLS : (e + 1) * EXP_COLS]
@@ -217,7 +245,7 @@ def tile_rbfnet_pb_t_kernel(
         sums = {}
 
         def scalar_empties(u):
-            return u >= 3 * TILE_UNITS or (u >= 2 * TILE_UNITS and u % 2 == 0)
+            return u >= 3 * TILE_UNITS or (u >= 2 * TILE_UNITS and u % TILE_UNITS in SHARED_UNITS)
 
         def invert_sum(jt):
             total = work.tile([P, 1], F32)
@@ -292,11 +320,16 @@ def tile_rbfnet_pb_t_kernel(
 
         def store(jt):
             out_sb = work.tile([P, C], F32)
-            nc.vector.tensor_copy(out=out_sb[:], in_=sums[jt][:])
+            if jt >= J_TILES - 2:
+                nc.scalar.copy(out=out_sb[:], in_=sums[jt][:])
+            else:
+                nc.vector.tensor_copy(out=out_sb[:], in_=sums[jt][:])
             nc.sync.dma_start(out=out[jt * P : (jt + 1) * P, :], in_=out_sb[:])
 
+        flip_x(0, nc.vector.tensor_copy)
         spread_s(0)
         spread_s(1)
+        quantise_x(0)
         distances((0, 1))
         kernel_values(0)
         kernel_values(1)
@@ -307,8 +340,8 @@ def tile_rbfnet_pb_t_kernel(
             first = jt * TILE_UNITS
             invert_sum(jt)
             for k in range(TILE_UNITS + LEAD + 1):
-                if jt == J_TILES - 2 and k % 2 == 1 and k // 2 < EXP_PIECES:
-                    kernel_piece(J_TILES - 1, k // 2)
+                if jt == J_TILES - 2 and k in EXP_STEPS:
+                    kernel_piece(J_TILES - 1, EXP_STEPS.index(k))
                 if k < TILE_UNITS:
                     normalise(first + k)
                     flip(first + k)

@@ -27,7 +27,6 @@ UNITS = J_TILES * TILE_UNITS
 LEAD = 2
 SHARED_UNITS = (0, 2, 3, 5)
 EXP_STEPS = (0, 3, 6, 8)
-BURST = 4
 CLAMP_COLS = 1024
 EXP_COLS = 2048
 EXP_PIECES = NTR // EXP_COLS
@@ -76,12 +75,6 @@ def tile_rbfnet_pb_t_kernel(
         make_identity(nc, ident_f32[:])
         nc.scalar.activation(out=warm[:, 1:2], in_=warm[:, 0:1], func=ACT.Sqrt)
 
-        nc.sync.dma_start(out=vec_rows[0:GROUPS, :], in_=s_norm2.rearrange("(g n) -> g n", g=GROUPS))
-        nc.sync.dma_start(
-            out=vec_rows[GROUPS : GROUPS + J_TILES, 0:P],
-            in_=c_norm2.rearrange("(a n) -> a n", a=J_TILES),
-        )
-
         def load_x(pair):
             nc.sync.dma_start(
                 out=x_sb[:, 2 * pair : 2 * pair + 2, :],
@@ -89,6 +82,11 @@ def tile_rbfnet_pb_t_kernel(
             )
 
         load_x(0)
+        nc.sync.dma_start(out=vec_rows[0:GROUPS, :], in_=s_norm2.rearrange("(g n) -> g n", g=GROUPS))
+        nc.sync.dma_start(
+            out=vec_rows[GROUPS : GROUPS + J_TILES, 0:P],
+            in_=c_norm2.rearrange("(a n) -> a n", a=J_TILES),
+        )
         for quadrant in range(4):
             nc.sync.dma_start(
                 out=sm_planes[32 * quadrant : 32 * quadrant + 16, :].bitcast(I32),
@@ -215,8 +213,8 @@ def tile_rbfnet_pb_t_kernel(
                 if batch[0] == 0:
                     if g == 0:
                         flip_x(1, nc.scalar.copy)
-                    if g + 2 < GROUPS // 2:
-                        spread_s(g + 2)
+                    if g % 2 == 0 and g // 2 + 2 < GROUPS // 2:
+                        spread_s(g // 2 + 2)
                     if g == 3:
                         quantise_x(1)
                 if (g + 1) * K_PASS in ends:
@@ -291,8 +289,8 @@ def tile_rbfnet_pb_t_kernel(
             packs[u] = w_grouped
 
         def quantise(u):
-            w_codes = work.tile([P, PAIR, P], U32, align_bytes=64, bufs=2 * BURST)
-            w_planes = work.tile([P, PAIR, P], U8, align_bytes=64, bufs=2 * BURST)
+            w_codes = work.tile([P, PAIR, P], U32, align_bytes=64, bufs=TILE_UNITS)
+            w_planes = work.tile([P, PAIR, P], U8, align_bytes=64, bufs=TILE_UNITS)
             nc.vector.quantize_mx(
                 out=w_codes[:].rearrange("p a j -> p (a j)").bitcast(FP8X4),
                 scales=w_planes[:].rearrange("p a j -> p (a j)"),
@@ -322,9 +320,10 @@ def tile_rbfnet_pb_t_kernel(
             out_sb = work.tile([P, C], F32)
             if jt >= J_TILES - 2:
                 nc.scalar.copy(out=out_sb[:], in_=sums[jt][:])
+                nc.scalar.dma_start(out=out[jt * P : (jt + 1) * P, :], in_=out_sb[:])
             else:
                 nc.vector.tensor_copy(out=out_sb[:], in_=sums[jt][:])
-            nc.sync.dma_start(out=out[jt * P : (jt + 1) * P, :], in_=out_sb[:])
+                nc.sync.dma_start(out=out[jt * P : (jt + 1) * P, :], in_=out_sb[:])
 
         flip_x(0, nc.vector.tensor_copy)
         spread_s(0)
@@ -350,7 +349,7 @@ def tile_rbfnet_pb_t_kernel(
                 if k - LEAD - 1 >= 0:
                     quantise(first + k - LEAD - 1)
                     waiting.append(first + k - LEAD - 1)
-                    if len(waiting) == BURST or k >= TILE_UNITS - 1:
+                    if k >= TILE_UNITS - 1:
                         for u in waiting:
                             multiply(u)
                         waiting.clear()

@@ -33,7 +33,8 @@ EXP_PIECES = NTR // EXP_COLS
 WORD_LOAD_COLS = 1024
 PLANE_COLS = NTR // 4
 SQRT_FLOOR = 2.0 ** -100
-SQRT_CEILING = 2.0 ** 118
+FAR = 3.0e38
+VECTOR_CLAMPS = (2048, 4096, 6144)
 
 FLOPS = 2 * NTR * NTE * D + 2 * NTE * NTR * C
 
@@ -64,6 +65,7 @@ def tile_rbfnet_pb_t_kernel(
         ident_f32 = keep.tile([P, P], F32)
         ident_bf16 = keep.tile([P, P], BF16)
         warm = keep.tile([P, 2], F32)
+        unused = keep.tile([P, 1], F32)
         k_sums = keep.tile([P, J_TILES, NTR // EXP_COLS], F32)
         k_tiles = [keep.tile([P, NTR], F32, name="k_tile%d" % jt) for jt in range(J_TILES)]
 
@@ -169,24 +171,35 @@ def tile_rbfnet_pb_t_kernel(
                 in_=x_grouped[:, 2 * pair * P * PACK : (2 * pair + 2) * P * PACK],
             )
 
-        def clamp_and_root(batch, begun, done):
-            for jt in batch:
-                piece = k_tiles[jt][:, begun:done]
+        def clamp_and_root(jt, begun, done, on_vector):
+            piece = k_tiles[jt][:, begun:done]
+            if on_vector:
+                nc.vector.tensor_scalar(
+                    out=piece,
+                    in0=piece,
+                    scalar1=-0.5 * SQRT_FLOOR,
+                    scalar2=None,
+                    op0=ALU.min,
+                    op1=ALU.max,
+                    accum_out=unused[:, 0:1],
+                )
+            else:
                 nc.gpsimd.tensor_scalar(
                     out=piece,
                     in0=piece,
                     scalar1=-0.5 * SQRT_FLOOR,
-                    scalar2=-0.5 * SQRT_CEILING,
+                    scalar2=-FAR,
                     op0=ALU.min,
                     op1=ALU.max,
                 )
-                nc.scalar.activation(out=piece, in_=piece, func=ACT.Sqrt, scale=-2.0)
+            nc.scalar.activation(out=piece, in_=piece, func=ACT.Sqrt, scale=-2.0)
 
         def distances(batch):
             ends = list(range(CLAMP_COLS, NTR + 1, CLAMP_COLS))
             if batch[0] == 0:
                 ends = [K_PASS] + ends + [NTR - K_PASS]
             begun = 0
+            late = []
             for g in range(GROUPS):
                 cols = slice(g * K_PASS, (g + 1) * K_PASS)
                 quarter, first = divmod(g * K_PASS, PLANE_COLS)
@@ -217,8 +230,15 @@ def tile_rbfnet_pb_t_kernel(
                         spread_s(g // 2 + 2)
                     if g == 3:
                         quantise_x(1)
+                for piece_of in late:
+                    clamp_and_root(piece_of[0], piece_of[1], piece_of[2], True)
+                late.clear()
                 if (g + 1) * K_PASS in ends:
-                    clamp_and_root(batch, begun, (g + 1) * K_PASS)
+                    for jt in batch:
+                        if jt == batch[1] and begun in VECTOR_CLAMPS:
+                            late.append((jt, begun, (g + 1) * K_PASS))
+                        else:
+                            clamp_and_root(jt, begun, (g + 1) * K_PASS, False)
                     begun = (g + 1) * K_PASS
 
         def kernel_piece(jt, e):

from contextlib import ExitStack

import concourse.mybir as mybir
from concourse.masks import make_identity

F32 = mybir.dt.float32
BF16 = mybir.dt.bfloat16
I32 = mybir.dt.int32
U32 = mybir.dt.uint32
U8 = mybir.dt.uint8
FP8X4 = mybir.dt.float8_e4m3fn_x4
ALU = mybir.AluOpType
ACT = mybir.ActivationFunctionType

P = 128
PACK = 4
K_PASS = P * PACK
NTR, NTE, D, C = 8192, 512, 512, 128
GAMMA = 10.0
J_TILES = NTE // P
GROUPS = NTR // K_PASS
PAIR = 2
UNIT_COLS = PAIR * K_PASS
UNIT_BLOCKS = UNIT_COLS // (2 * P)
TILE_UNITS = NTR // UNIT_COLS
UNITS = J_TILES * TILE_UNITS
LEAD = 2
SHARED_UNITS = (0, 2, 3, 5)
EXP_STEPS = (0, 3, 6, 8)
CLAMP_COLS = 1024
EXP_COLS = 2048
EXP_PIECES = NTR // EXP_COLS
WORD_LOAD_COLS = 1024
PLANE_COLS = NTR // 4
SQRT_FLOOR = 2.0 ** -100
FAR = 3.0e38
VECTOR_CLAMPS = (2048, 4096, 6144)

FLOPS = 2 * NTR * NTE * D + 2 * NTE * NTR * C


def tile_rbfnet_pb_t_kernel(
    tc, sM_words, sM_scales, x_test, s_norm2, c_norm2, y_train_words, y_train_scales, out
):
    nc = tc.nc
    with ExitStack() as ctx:
        keep = ctx.enter_context(tc.tile_pool(name="keep", bufs=1))
        work = ctx.enter_context(tc.tile_pool(name="work", bufs=2))
        psum_ring = ctx.enter_context(tc.psum_pool(name="psum_ring", bufs=6))
        psum_sums = ctx.enter_context(tc.psum_pool(name="psum_sums", bufs=2))
        ctx.enter_context(tc.manual_schedule())

        x_sb = keep.tile([P, J_TILES, D], BF16)
        x_grouped = keep.tile([P, NTE * PACK], BF16, align_bytes=64)
        x_codes = keep.tile([P, NTE], U32, align_bytes=64)
        x_planes = keep.tile([P, NTE], U8, align_bytes=64)
        sm_codes = keep.tile([P, NTR], U32, align_bytes=64)
        sm_planes = keep.tile([P, PLANE_COLS], U8, align_bytes=64)
        y_codes = keep.tile([P, GROUPS, C], U32, align_bytes=64)
        y_planes = keep.tile([P, GROUPS, C], U8, align_bytes=64)
        vec_rows = keep.tile([P, K_PASS], BF16)
        s_cols = keep.tile([P, GROUPS, PACK], BF16)
        c_cols = keep.tile([P, J_TILES], F32)
        s_all = keep.tile([P, GROUPS, PACK, P], BF16)
        ident_f32 = keep.tile([P, P], F32)
        ident_bf16 = keep.tile([P, P], BF16)
        warm = keep.tile([P, 2], F32)
        unused = keep.tile([P, 1], F32)
        k_sums = keep.tile([P, J_TILES, NTR // EXP_COLS], F32)
        k_tiles = [keep.tile([P, NTR], F32, name="k_tile%d" % jt) for jt in range(J_TILES)]

        nc.vector.memset(vec_rows[:], 0.0)
        nc.vector.memset(sm_planes[:].bitcast(I32), 0)
        nc.vector.memset(warm[:], 1.0)
        nc.vector.memset(y_planes[:].rearrange("p g c -> p (g c)").bitcast(I32), 0)
        make_identity(nc, ident_bf16[:])
        make_identity(nc, ident_f32[:])
        nc.scalar.activation(out=warm[:, 1:2], in_=warm[:, 0:1], func=ACT.Sqrt)

        def load_x(pair):
            nc.sync.dma_start(
                out=x_sb[:, 2 * pair : 2 * pair + 2, :],
                in_=x_test[2 * pair * P : (2 * pair + 2) * P, :].rearrange("(a p) k -> p a k", p=P),
            )

        load_x(0)
        nc.sync.dma_start(out=vec_rows[0:GROUPS, :], in_=s_norm2.rearrange("(g n) -> g n", g=GROUPS))
        nc.sync.dma_start(
            out=vec_rows[GROUPS : GROUPS + J_TILES, 0:P],
            in_=c_norm2.rearrange("(a n) -> a n", a=J_TILES),
        )
        for quadrant in range(4):
            nc.sync.dma_start(
                out=sm_planes[32 * quadrant : 32 * quadrant + 16, :].bitcast(I32),
                in_=sM_scales[0, 4 * quadrant : 4 * quadrant + 4, :]
                .rearrange("r (v n) -> v r n", v=4)
                .bitcast(I32),
            )
        sm_word_bytes = sM_words.rearrange("o p n t -> (o p) (n t)")
        for first in range(0, NTR, WORD_LOAD_COLS):
            nc.sync.dma_start(
                out=sm_codes[:, first : first + WORD_LOAD_COLS].bitcast(I32),
                in_=sm_word_bytes[:, PACK * first : PACK * (first + WORD_LOAD_COLS)].bitcast(I32),
            )
            if first == 0:
                load_x(1)
        for quadrant in range(4):
            nc.sync.dma_start(
                out=y_planes[32 * quadrant : 32 * quadrant + 4, :, :].bitcast(I32),
                in_=y_train_scales[:, 4 * quadrant : 4 * quadrant + 4, :]
                .rearrange("g r n -> r g n")
                .bitcast(I32),
            )
        nc.sync.dma_start(
            out=y_codes[:].bitcast(I32),
            in_=y_train_words.rearrange("g p n t -> p g (n t)").bitcast(I32),
        )

        vec_flip = psum_ring.tile([P, PACK + 1, P], BF16, tag="ring")
        for t in range(PACK):
            nc.tensor.transpose(vec_flip[:, t, :], vec_rows[:, t:K_PASS:PACK], ident_bf16[:])
        nc.tensor.transpose(vec_flip[:, PACK, :], vec_rows[:, 0:P], ident_bf16[:])
        nc.vector.tensor_scalar(
            out=s_cols[:],
            in0=vec_flip[:, 0:PACK, 0:GROUPS].rearrange("p t g -> p g t"),
            scalar1=0.5,
            scalar2=None,
            op0=ALU.mult,
        )
        nc.vector.tensor_scalar(
            out=c_cols[:],
            in0=vec_flip[:, PACK, GROUPS : GROUPS + J_TILES],
            scalar1=0.5,
            scalar2=None,
            op0=ALU.mult,
        )

        def spread_s(pair):
            s_bank = psum_ring.tile([P, 2, PACK, P], BF16, tag="ring")
            for a in range(2):
                for t in range(PACK):
                    nc.tensor.matmul(
                        out=s_bank[:, a, t, :],
                        lhsT=s_cols[:, 2 * pair + a, t : t + 1].to_broadcast([P, P]),
                        rhs=ident_bf16[:],
                        start=True,
                        stop=True,
                    )
            nc.scalar.copy(out=s_all[:, 2 * pair : 2 * pair + 2, :, :], in_=s_bank[:])

        x_grouped_words = x_grouped[:].bitcast(F32).rearrange("p (a j u) -> p a j u", a=J_TILES, u=2)

        def flip_x(pair, copy_out):
            x_flip = psum_ring.tile([P, 2, 2, P], F32, tag="ring")
            for a in range(2):
                for u in range(2):
                    nc.tensor.transpose(
                        x_flip[:, a, u, :],
                        x_sb[:, 2 * pair + a, :].bitcast(F32)[:, u : D // 2 : 2],
                        ident_f32[:],
                    )
            copy_out(
                out=x_grouped_words[:, 2 * pair : 2 * pair + 2, :, :],
                in_=x_flip[:].rearrange("p a u j -> p a j u"),
            )

        def quantise_x(pair):
            nc.vector.quantize_mx(
                out=x_codes[:, 2 * pair * P : (2 * pair + 2) * P].bitcast(FP8X4),
                scales=x_planes[:, 2 * pair * P : (2 * pair + 2) * P],
                in_=x_grouped[:, 2 * pair * P * PACK : (2 * pair + 2) * P * PACK],
            )

        def clamp_and_root(jt, begun, done, on_vector):
            piece = k_tiles[jt][:, begun:done]
            if on_vector:
                nc.vector.tensor_scalar(
                    out=piece,
                    in0=piece,
                    scalar1=-0.5 * SQRT_FLOOR,
                    scalar2=None,
                    op0=ALU.min,
                    op1=ALU.max,
                    accum_out=unused[:, 0:1],
                )
            else:
                nc.gpsimd.tensor_scalar(
                    out=piece,
                    in0=piece,
                    scalar1=-0.5 * SQRT_FLOOR,
                    scalar2=-FAR,
                    op0=ALU.min,
                    op1=ALU.max,
                )
            nc.scalar.activation(out=piece, in_=piece, func=ACT.Sqrt, scale=-2.0)

        def distances(batch):
            ends = list(range(CLAMP_COLS, NTR + 1, CLAMP_COLS))
            if batch[0] == 0:
                ends = [K_PASS] + ends + [NTR - K_PASS]
            begun = 0
            late = []
            for g in range(GROUPS):
                cols = slice(g * K_PASS, (g + 1) * K_PASS)
                quarter, first = divmod(g * K_PASS, PLANE_COLS)
                plane_cols = slice(first, first + K_PASS)
                for jt in batch:
                    cross = psum_ring.tile([P, K_PASS], F32, tag="ring")
                    nc.tensor.matmul_mx(
                        out=cross[:],
                        lhsT=x_codes[:, jt * P : (jt + 1) * P].bitcast(FP8X4),
                        lhsT_scale=x_planes[:, jt * P : (jt + 1) * P],
                        rhs=sm_codes[:, cols].bitcast(FP8X4),
                        rhs_scale=sm_planes[PACK * quarter : P, plane_cols],
                        start=True,
                        stop=True,
                    )
                    nc.vector.scalar_tensor_tensor(
                        out=k_tiles[jt][:, cols].rearrange("p (t n) -> p t n", t=PACK),
                        in0=cross[:].rearrange("p (n t) -> p t n", t=PACK),
                        scalar=c_cols[:, jt : jt + 1],
                        in1=s_all[:, g, :, :],
                        op0=ALU.subtract,
                        op1=ALU.subtract,
                    )
                if batch[0] == 0:
                    if g == 0:
                        flip_x(1, nc.scalar.copy)
                    if g % 2 == 0 and g // 2 + 2 < GROUPS // 2:
                        spread_s(g // 2 + 2)
                    if g == 3:
                        quantise_x(1)
                for piece_of in late:
                    clamp_and_root(piece_of[0], piece_of[1], piece_of[2], True)
                late.clear()
                if (g + 1) * K_PASS in ends:
                    for jt in batch:
                        if jt == batch[1] and begun in VECTOR_CLAMPS:
                            late.append((jt, begun, (g + 1) * K_PASS))
                        else:
                            clamp_and_root(jt, begun, (g + 1) * K_PASS, False)
                    begun = (g + 1) * K_PASS

        def kernel_piece(jt, e):
            piece = k_tiles[jt][:, e * EXP_COLS : (e + 1) * EXP_COLS]
            nc.scalar.activation(
                out=piece,
                in_=piece,
                func=ACT.Exp,
                scale=-1.0 / GAMMA,
                accum_out=k_sums[:, jt, e : e + 1],
            )

        def kernel_values(jt):
            for e in range(EXP_PIECES):
                kernel_piece(jt, e)

        inverses = {}
        pairs = {}
        flips = {}
        packs = {}
        codes = {}
        sums = {}

        def scalar_empties(u):
            return u >= 3 * TILE_UNITS or (u >= 2 * TILE_UNITS and u % TILE_UNITS in SHARED_UNITS)

        def invert_sum(jt):
            total = work.tile([P, 1], F32)
            nc.vector.reduce_sum(out=total[:], in_=k_sums[:, jt, :], axis=mybir.AxisListType.X)
            inverse = work.tile([P, 1], F32)
            nc.vector.reciprocal(out=inverse[:], in_=total[:])
            inverses[jt] = inverse

        def normalise(u):
            jt, h = divmod(u, TILE_UNITS)
            w_pairs = work.tile([P, UNIT_COLS], BF16, bufs=LEAD + 2)
            nc.vector.tensor_scalar(
                out=w_pairs[:].rearrange("p (b n e) -> p b n e", b=UNIT_BLOCKS, e=2),
                in0=k_tiles[jt][:, h * UNIT_COLS : (h + 1) * UNIT_COLS].rearrange(
                    "p (b e n) -> p b n e", b=UNIT_BLOCKS, e=2
                ),
                scalar1=inverses[jt][:, 0:1],
                scalar2=None,
                op0=ALU.mult,
            )
            pairs[u] = w_pairs

        def flip(u):
            w_flip = psum_ring.tile([P, UNIT_BLOCKS, P], F32, tag="ring")
            words = pairs[u][:].bitcast(F32)
            for b in range(UNIT_BLOCKS):
                nc.tensor.transpose(w_flip[:, b, :], words[:, b * P : (b + 1) * P], ident_f32[:])
            flips[u] = w_flip

        def empty(u):
            w_grouped = work.tile([P, PAIR, P, PACK], BF16, align_bytes=64, bufs=4)
            target = (
                w_grouped[:]
                .rearrange("p a j t -> p (a j t)")
                .bitcast(F32)
                .rearrange("p (a j u) -> p a j u", a=PAIR, u=2)
            )
            source = flips[u][:].rearrange("p (a u) j -> p a j u", u=2)
            if scalar_empties(u):
                nc.scalar.copy(out=target, in_=source)
            else:
                nc.vector.tensor_copy(out=target, in_=source)
            packs[u] = w_grouped

        def quantise(u):
            w_codes = work.tile([P, PAIR, P], U32, align_bytes=64, bufs=TILE_UNITS)
            w_planes = work.tile([P, PAIR, P], U8, align_bytes=64, bufs=TILE_UNITS)
            nc.vector.quantize_mx(
                out=w_codes[:].rearrange("p a j -> p (a j)").bitcast(FP8X4),
                scales=w_planes[:].rearrange("p a j -> p (a j)"),
                in_=packs[u][:].rearrange("p a j t -> p (a j t)"),
            )
            codes[u] = (w_codes, w_planes)

        def multiply(u):
            jt, h = divmod(u, TILE_UNITS)
            w_codes, w_planes = codes[u]
            if h == 0:
                out_acc = psum_sums.tile([P, C], F32)
                sums[jt] = out_acc
            for a in range(PAIR):
                g = PAIR * h + a
                nc.tensor.matmul_mx(
                    out=sums[jt][:],
                    lhsT=w_codes[:, a, :].bitcast(FP8X4),
                    lhsT_scale=w_planes[:, a, :],
                    rhs=y_codes[:, g, :].bitcast(FP8X4),
                    rhs_scale=y_planes[:, g, :],
                    start=(g == 0),
                    stop=(g == GROUPS - 1),
                )

        def store(jt):
            out_sb = work.tile([P, C], F32)
            if jt >= J_TILES - 2:
                nc.scalar.copy(out=out_sb[:], in_=sums[jt][:])
                nc.scalar.dma_start(out=out[jt * P : (jt + 1) * P, :], in_=out_sb[:])
            else:
                nc.vector.tensor_copy(out=out_sb[:], in_=sums[jt][:])
                nc.sync.dma_start(out=out[jt * P : (jt + 1) * P, :], in_=out_sb[:])

        flip_x(0, nc.vector.tensor_copy)
        spread_s(0)
        spread_s(1)
        quantise_x(0)
        distances((0, 1))
        kernel_values(0)
        kernel_values(1)
        distances((2, 3))
        kernel_values(2)
        waiting = []
        for jt in range(J_TILES):
            first = jt * TILE_UNITS
            invert_sum(jt)
            for k in range(TILE_UNITS + LEAD + 1):
                if jt == J_TILES - 2 and k in EXP_STEPS:
                    kernel_piece(J_TILES - 1, EXP_STEPS.index(k))
                if k < TILE_UNITS:
                    normalise(first + k)
                    flip(first + k)
                if 0 <= k - LEAD < TILE_UNITS:
                    empty(first + k - LEAD)
                if k - LEAD - 1 >= 0:
                    quantise(first + k - LEAD - 1)
                    waiting.append(first + k - LEAD - 1)
                    if k >= TILE_UNITS - 1:
                        for u in waiting:
                            multiply(u)
                        waiting.clear()
            store(jt)
